import numpy as np
import ml_dtypes


def mxq(x, axis, fmt="e4m3"):
    dtype, down = {"e4m3": (ml_dtypes.float8_e4m3fn, 7), "e5m2": (ml_dtypes.float8_e5m2, 14)}[fmt]
    v = np.moveaxis(np.asarray(x, np.float32).astype(ml_dtypes.bfloat16).astype(np.float64), axis, -1)
    blocks = v.reshape(v.shape[:-1] + (-1, 32))
    amax = np.abs(blocks).max(-1, keepdims=True)
    byte = np.maximum(np.where(amax > 0, np.frexp(amax)[1] - 1 + 127, 0) - down, 1)
    scale = np.exp2(byte - 127.0)
    codes = (blocks / scale).astype(np.float32).astype(dtype).astype(np.float64)
    return np.moveaxis((codes * scale).reshape(v.shape), -1, axis)


WIDE = False


def mx_kscale(k):
    if not WIDE:
        return np.ones(k)
    levels = np.array([10, -10, 5, -5, 0])
    a = np.random.permutation(np.resize(levels, k // 512 * 4)).reshape(k // 512, 4)
    idx = np.arange(k)
    return np.exp2(a[idx // 512, idx % 128 // 32])


BF16 = ml_dtypes.bfloat16


def bf(x):
    return np.asarray(x, np.float32).astype(BF16)


def f64(x):
    return np.asarray(x).astype(np.float64)


B, C, LL, LM, LS = 256, 256, 10, 20, 30
SOFTMAX_SCALE = 10.0


def softmax(v, axis):
    e = np.exp(v - v.max(axis=axis, keepdims=True))
    return e / e.sum(axis=axis, keepdims=True)


def setup_inputs():
    s = mx_kscale(2 * C)[:C][None, :, None]
    g = lambda l: np.random.standard_normal((B, C, l))
    return {"left": bf(g(LL) * 0.3 / np.sqrt(2 * C) / s), "right": bf(g(LL) * 0.3 / np.sqrt(2 * C) / s), "mid": bf(g(LM) * s),
            "sc00": bf(g(LS) * 0.1), "sc01": bf(g(LS) * 0.1), "sc10": bf(g(LS) * 0.1), "sc11": bf(g(LS) * 0.1)}


def reference(left, right, mid, sc00, sc01, sc10, sc11):
    left, right, mid, sc00, sc01, sc10, sc11 = (f64(a) for a in (left, right, mid, sc00, sc01, sc10, sc11))
    b, c, lm = mid.shape
    left_cat = np.concatenate([left, right], axis=2)
    raw_l = [np.concatenate([sc00, sc10], axis=2), sc10]
    lcat = left_cat.shape[2]
    n = min(-(-lm // 2), -(-lcat // 2), b)
    X = mid[:, :, : 2 * n].reshape(b, c, n, 2).transpose(2, 0, 1, 3)
    X = np.pad(X, ((0, 0), (0, 0), (0, 0), (1, 0)))
    W = left_cat[:, :, : 2 * n].reshape(b, c, n, 2).transpose(2, 0, 1, 3)
    win = np.stack([X[..., 0:2], X[..., 1:3]], axis=3)
    A = win.transpose(0, 1, 3, 4, 2).reshape(n, b * 2, 2 * c)
    Wm = W.transpose(0, 3, 2, 1).reshape(n, 2 * c, b)
    scores = (mxq(A, 2, "e4m3") @ mxq(Wm, 1, "e4m3")) * SOFTMAX_SCALE
    scores = scores.reshape(n, b, 2, b).transpose(0, 1, 3, 2)
    att = softmax(scores, 2)
    att = np.pad(att, ((0, 0), (0, 0), (0, c - b), (0, 0)))
    ls = sc10.shape[2]
    outs = []
    for rl in raw_l:
        centers = np.moveaxis(rl[:, :, :n], 2, 0)[..., None]
        y = np.concatenate([att, centers], axis=3)
        y = np.moveaxis(y, 0, 2).reshape(b, c, 3 * n)
        pad = ls - y.shape[2]
        if pad > 0:
            y = np.pad(y, ((0, 0), (0, 0), (0, pad)))
        outs.append(y)
    return tuple(outs)

@@ -1,0 +1,168 @@
+from contextlib import ExitStack
+
+import concourse.mybir as mybir
+from concourse.masks import make_identity
+
+F32 = mybir.dt.float32
+BF16 = mybir.dt.bfloat16
+U32 = mybir.dt.uint32
+U8 = mybir.dt.uint8
+FP8X4 = mybir.dt.float8_e4m3fn_x4
+ACT = mybir.ActivationFunctionType
+ALU = mybir.AluOpType
+AX = mybir.AxisListType
+
+P = 128
+NCHUNK = 10
+FLOPS = 2 * 5120 * 256 * 512
+BYTES = 2 * 256 * 256 * 30 * 4 + 2 * 256 * 256 * 20 * 2 + 2 * 256 * 256 * 10 * 2
+
+RUN = 4
+V_GROUPS = 20
+G0_ON_GPSIMD = True
+
+
+def tile_contextualattention_t_kernel(tc, left, right, mid, sc00, sc01, sc10, sc11, out_0, out_1):
+    nc = tc.nc
+    outs = (out_0, out_1)
+    with ExitStack() as ctx:
+        const = ctx.enter_context(tc.tile_pool(name="const", bufs=1))
+        ins = ctx.enter_context(tc.tile_pool(name="ins", bufs=1))
+        slots = ctx.enter_context(tc.tile_pool(name="slots", bufs=6))
+        srcp = ctx.enter_context(tc.tile_pool(name="srcp", bufs=2))
+        keep = ctx.enter_context(tc.tile_pool(name="keep", bufs=1))
+        gp = ctx.enter_context(tc.tile_pool(name="gp", bufs=2))
+        mp = ctx.enter_context(tc.tile_pool(name="mp", bufs=3))
+        small = ctx.enter_context(tc.tile_pool(name="small", bufs=4))
+        stat = ctx.enter_context(tc.tile_pool(name="stat", bufs=2))
+        xtp = ctx.enter_context(tc.psum_pool(name="xtp", bufs=3))
+        scp = ctx.enter_context(tc.psum_pool(name="scp", bufs=4))
+
+        ident = const.tile([P, P], F32, name="ident")
+        make_identity(nc, ident[:])
+
+        left_sb = ins.tile([P, 2, 2560], BF16, name="left_sb")
+        right_sb = ins.tile([P, 2, 2560], BF16, name="right_sb")
+        mid_sb = [ins.tile([P, 5120], BF16, name="mid_sb%d" % h) for h in range(2)]
+        nc.sync.dma_start(out=left_sb[:], in_=left.rearrange("(q o) c l -> o q (c l)", q=2))
+        nc.sync.dma_start(out=mid_sb[0][:], in_=mid[0:P].rearrange("b c l -> b (c l)"))
+        nc.sync.dma_start(out=right_sb[:], in_=right.rearrange("(q o) c l -> o q (c l)", q=2))
+        nc.sync.dma_start(out=mid_sb[1][:], in_=mid[P:2 * P].rearrange("b c l -> b (c l)"))
+        sc_sb = {}
+        for h in range(2):
+            for x, sc in enumerate((sc00, sc10)):
+                t = slots.tile([P, 7680], BF16, tag="slot", name="sc_sb%d%d" % (x, h))
+                nc.sync.dma_start(out=t[:], in_=sc[h * P:(h + 1) * P].rearrange("b c l -> b (c l)"))
+                sc_sb[(x, h)] = t
+
+        lc_codes = keep.tile([P, NCHUNK, 256], U32, name="lc_codes", align_bytes=64)
+        lc_scales = keep.tile([P, NCHUNK, 256], U8, name="lc_scales", align_bytes=64)
+
+        def lc_unit(i):
+            sb = left_sb if i < 5 else right_sb
+            words = sb[:].bitcast(F32).rearrange("p q (m u i) -> p q m u i", u=2, i=5)
+            xt = xtp.tile([P, 2, 256], F32, tag="xt", name="xt_lc")
+            for u in range(2):
+                for q in range(2):
+                    nc.tensor.transpose(out=xt[:, u, q * P:(q + 1) * P], in_=words[:, q, :, u, i % 5], identity=ident[:])
+            g = gp.tile([P, 1024], BF16, tag="g_lc", name="g_lc", align_bytes=64)
+            nc.vector.tensor_copy(
+                out=g[:].bitcast(F32).rearrange("p (o u) -> p o u", u=2),
+                in_=xt[:].rearrange("p u o -> p o u"),
+            )
+            nc.vector.quantize_mx(out=lc_codes[:, i, :].bitcast(FP8X4), scales=lc_scales[:, i, :], in_=g[:])
+
+        def mid_unit(h, k):
+            words = mid_sb[h][:].bitcast(F32).rearrange("p (m u i) -> p m u i", u=2, i=10)
+            xt = xtp.tile([P, 2, 2, P], F32, tag="xt", name="xt_mid")
+            for x in range(2):
+                for u in range(2):
+                    nc.tensor.transpose(out=xt[:, x, u, :], in_=words[:, :, u, 2 * k + x], identity=ident[:])
+            g = gp.tile([P, 2048], BF16, tag="g_mid", name="g_mid", align_bytes=64)
+            gw = g[:].bitcast(F32).rearrange("p (v x b u) -> p v x b u", v=2, x=2, u=2)
+            nc.scalar.copy(out=gw[:, 0], in_=xt[:].rearrange("p x u b -> p x b u"))
+            if G0_ON_GPSIMD:
+                first = g[:, 0:1024].rearrange("p (w e) -> p w e", e=2)[:, :, 0]
+                nc.gpsimd.tensor_scalar(
+                    out=g[:, 1024:2048].bitcast(F32), in0=first, scalar1=1.0, scalar2=0.0, op0=ALU.mult, op1=ALU.add
+                )
+            else:
+                tap0 = xt[:].bitcast(BF16).rearrange("p x u (b e) -> p x b u e", e=2)[:, :, :, :, 0]
+                nc.scalar.copy(out=gw[:, 1], in_=tap0)
+            codes = mp.tile([P, 512], U32, tag="m_codes", name="m_codes", align_bytes=64)
+            scales = mp.tile([P, 512], U8, tag="m_scales", name="m_scales", align_bytes=64)
+            nc.vector.quantize_mx(out=codes[:].bitcast(FP8X4), scales=scales[:], in_=g[:])
+            return codes, scales
+
+        def scores(src_t, sums, rinv, i, codes, scales):
+            x = i % 2
+            ps = scp.tile([P, 2, 256], F32, tag="ps", name="ps")
+            for t in range(2):
+                c0 = ((1 - t) * 2 + x) * P
+                nc.tensor.matmul_mx(
+                    out=ps[:, t, :],
+                    lhsT=codes[:, c0:c0 + P].bitcast(FP8X4),
+                    lhsT_scale=scales[:, c0:c0 + P],
+                    rhs=lc_codes[:, i, :].bitcast(FP8X4),
+                    rhs_scale=lc_scales[:, i, :],
+                    start=True,
+                    stop=True,
+                )
+            mx = small.tile([P, 2], F32, tag="mx", name="mx")
+            nc.vector.reduce_max(out=mx[:], in_=ps[:], axis=AX.X)
+            nb = small.tile([P, 2], F32, tag="nb", name="nb")
+            nc.vector.tensor_scalar_mul(out=nb[:], in0=mx[:], scalar1=-10.0)
+            for t in range(2):
+                nc.scalar.activation(
+                    out=src_t[:, :, i, t, :],
+                    in_=ps[:, t, :].rearrange("p (q o) -> p q o", q=2),
+                    func=ACT.Exp,
+                    bias=nb[:, t:t + 1],
+                    scale=10.0,
+                    accum_out=sums[:, 2 * i + t:2 * i + t + 1],
+                )
+            nc.vector.reciprocal(out=rinv[:, 2 * i:2 * i + 2], in_=sums[:, 2 * i:2 * i + 2])
+            for t in range(2):
+                nc.vector.tensor_scalar_mul(
+                    out=src_t[:, :, i, t, :], in0=src_t[:, :, i, t, :], scalar1=rinv[:, 2 * i + t:2 * i + t + 1]
+                )
+
+        def centers(src_t, x, h, q):
+            scv = sc_sb[(x, h)][:].rearrange("p (q o l) -> p q o l", q=2, l=30)
+            nc.gpsimd.tensor_scalar(
+                out=src_t[:, q, :, 2, :].rearrange("p (g e) o -> p g o e", e=2),
+                in0=scv[:, q, :, 0:10].rearrange("p o (g e) -> p g o e", e=2),
+                scalar1=1.0,
+                scalar2=0.0,
+                op0=ALU.mult,
+                op1=ALU.add,
+            )
+
+        def assemble(src_t, x, h, q):
+            o_t = slots.tile([P, 3840], F32, tag="slot", name="o_t")
+            dst = o_t[:].rearrange("p (a e j) -> p a j e", e=RUN, j=30)
+            srcv = src_t[:, q].rearrange("p i r (a e) -> p a (i r) e", e=RUN)
+            nc.vector.tensor_copy(out=dst[:, 0:V_GROUPS], in_=srcv[:, 0:V_GROUPS])
+            nc.scalar.copy(out=dst[:, V_GROUPS:], in_=srcv[:, V_GROUPS:])
+            nc.sync.dma_start(
+                out=outs[x][h * P:(h + 1) * P, q * P:(q + 1) * P, :].rearrange("b o j -> b (o j)"), in_=o_t[:]
+            )
+
+        for h in range(2):
+            src_t = srcp.tile([P, 2, NCHUNK, 3, P], F32, tag="src", name="src_t")
+            sums = stat.tile([P, 2 * NCHUNK], F32, tag="sums", name="sums")
+            rinv = stat.tile([P, 2 * NCHUNK], F32, tag="rinv", name="rinv")
+            for k in range(5):
+                if h == 0:
+                    lc_unit(2 * k)
+                    lc_unit(2 * k + 1)
+                codes, scales = mid_unit(h, k)
+                scores(src_t, sums, rinv, 2 * k, codes, scales)
+                scores(src_t, sums, rinv, 2 * k + 1, codes, scales)
+            for q in range(2):
+                centers(src_t, 0, h, q)
+            for q in range(2):
+                assemble(src_t, 0, h, q)
+                centers(src_t, 1, h, q)
+            for q in range(2):
+                assemble(src_t, 1, h, q)

@@ -18,8 +18,7 @@ FLOPS = 2 * 5120 * 256 * 512
 BYTES = 2 * 256 * 256 * 30 * 4 + 2 * 256 * 256 * 20 * 2 + 2 * 256 * 256 * 10 * 2
 
 RUN = 4
-V_GROUPS = 20
-G0_ON_GPSIMD = True
+V_GROUPS = 22
 
 
 def tile_contextualattention_t_kernel(tc, left, right, mid, sc00, sc01, sc10, sc11, out_0, out_1):
@@ -33,10 +32,11 @@ def tile_contextualattention_t_kernel(tc, left, right, mid, sc00, sc01, sc10, sc
         keep = ctx.enter_context(tc.tile_pool(name="keep", bufs=1))
         gp = ctx.enter_context(tc.tile_pool(name="gp", bufs=2))
         mp = ctx.enter_context(tc.tile_pool(name="mp", bufs=3))
-        small = ctx.enter_context(tc.tile_pool(name="small", bufs=4))
+        small = ctx.enter_context(tc.tile_pool(name="small", bufs=6))
         stat = ctx.enter_context(tc.tile_pool(name="stat", bufs=2))
-        xtp = ctx.enter_context(tc.psum_pool(name="xtp", bufs=3))
+        xtp = ctx.enter_context(tc.psum_pool(name="xtp", bufs=4))
         scp = ctx.enter_context(tc.psum_pool(name="scp", bufs=4))
+        ctx.enter_context(tc.manual_schedule())
 
         ident = const.tile([P, P], F32, name="ident")
         make_identity(nc, ident[:])
@@ -57,77 +57,111 @@ def tile_contextualattention_t_kernel(tc, left, right, mid, sc00, sc01, sc10, sc
 
         lc_codes = keep.tile([P, NCHUNK, 256], U32, name="lc_codes", align_bytes=64)
         lc_scales = keep.tile([P, NCHUNK, 256], U8, name="lc_scales", align_bytes=64)
+        state = {}
 
-        def lc_unit(i):
-            sb = left_sb if i < 5 else right_sb
-            words = sb[:].bitcast(F32).rearrange("p q (m u i) -> p q m u i", u=2, i=5)
-            xt = xtp.tile([P, 2, 256], F32, tag="xt", name="xt_lc")
-            for u in range(2):
-                for q in range(2):
-                    nc.tensor.transpose(out=xt[:, u, q * P:(q + 1) * P], in_=words[:, q, :, u, i % 5], identity=ident[:])
-            g = gp.tile([P, 1024], BF16, tag="g_lc", name="g_lc", align_bytes=64)
-            nc.vector.tensor_copy(
-                out=g[:].bitcast(F32).rearrange("p (o u) -> p o u", u=2),
-                in_=xt[:].rearrange("p u o -> p o u"),
-            )
-            nc.vector.quantize_mx(out=lc_codes[:, i, :].bitcast(FP8X4), scales=lc_scales[:, i, :], in_=g[:])
-
-        def mid_unit(h, k):
-            words = mid_sb[h][:].bitcast(F32).rearrange("p (m u i) -> p m u i", u=2, i=10)
-            xt = xtp.tile([P, 2, 2, P], F32, tag="xt", name="xt_mid")
-            for x in range(2):
+        def prep_t(unit):
+            kind, a, b = unit
+            if kind == "L":
+                sb = left_sb if a < 5 else right_sb
+                words = sb[:].bitcast(F32).rearrange("p q (m u i) -> p q m u i", u=2, i=5)
+                xt = xtp.tile([P, 2, 256], F32, tag="xt", name="xt_lc")
                 for u in range(2):
-                    nc.tensor.transpose(out=xt[:, x, u, :], in_=words[:, :, u, 2 * k + x], identity=ident[:])
-            g = gp.tile([P, 2048], BF16, tag="g_mid", name="g_mid", align_bytes=64)
-            gw = g[:].bitcast(F32).rearrange("p (v x b u) -> p v x b u", v=2, x=2, u=2)
-            nc.scalar.copy(out=gw[:, 0], in_=xt[:].rearrange("p x u b -> p x b u"))
-            if G0_ON_GPSIMD:
-                first = g[:, 0:1024].rearrange("p (w e) -> p w e", e=2)[:, :, 0]
-                nc.gpsimd.tensor_scalar(
-                    out=g[:, 1024:2048].bitcast(F32), in0=first, scalar1=1.0, scalar2=0.0, op0=ALU.mult, op1=ALU.add
-                )
+                    for q in range(2):
+                        nc.tensor.transpose(out=xt[:, u, q * P:(q + 1) * P], in_=words[:, q, :, u, a % 5], identity=ident[:])
             else:
+                words = mid_sb[a][:].bitcast(F32).rearrange("p (m u i) -> p m u i", u=2, i=10)
+                xt = xtp.tile([P, 2, 2, P], F32, tag="xt", name="xt_mid")
+                for x in range(2):
+                    for u in range(2):
+                        nc.tensor.transpose(out=xt[:, x, u, :], in_=words[:, :, u, 2 * b + x], identity=ident[:])
+            state[("xt", unit)] = xt
+
+        def prep_e(unit):
+            kind, a, b = unit
+            xt = state[("xt", unit)]
+            if kind == "L":
+                g = gp.tile([P, 1024], BF16, tag="g_lc", name="g_lc", align_bytes=64)
+                nc.scalar.copy(out=g[:].bitcast(F32).rearrange("p (o u) -> p o u", u=2), in_=xt[:].rearrange("p u o -> p o u"))
+            else:
+                g = gp.tile([P, 2048], BF16, tag="g_mid", name="g_mid", align_bytes=64)
+                gw = g[:].bitcast(F32).rearrange("p (v x b u) -> p v x b u", v=2, x=2, u=2)
+                nc.scalar.copy(out=gw[:, 0], in_=xt[:].rearrange("p x u b -> p x b u"))
                 tap0 = xt[:].bitcast(BF16).rearrange("p x u (b e) -> p x b u e", e=2)[:, :, :, :, 0]
                 nc.scalar.copy(out=gw[:, 1], in_=tap0)
-            codes = mp.tile([P, 512], U32, tag="m_codes", name="m_codes", align_bytes=64)
-            scales = mp.tile([P, 512], U8, tag="m_scales", name="m_scales", align_bytes=64)
-            nc.vector.quantize_mx(out=codes[:].bitcast(FP8X4), scales=scales[:], in_=g[:])
-            return codes, scales
+            state[("g", unit)] = g
 
-        def scores(src_t, sums, rinv, i, codes, scales):
-            x = i % 2
-            ps = scp.tile([P, 2, 256], F32, tag="ps", name="ps")
-            for t in range(2):
-                c0 = ((1 - t) * 2 + x) * P
-                nc.tensor.matmul_mx(
-                    out=ps[:, t, :],
-                    lhsT=codes[:, c0:c0 + P].bitcast(FP8X4),
-                    lhsT_scale=scales[:, c0:c0 + P],
-                    rhs=lc_codes[:, i, :].bitcast(FP8X4),
-                    rhs_scale=lc_scales[:, i, :],
-                    start=True,
-                    stop=True,
-                )
-            mx = small.tile([P, 2], F32, tag="mx", name="mx")
-            nc.vector.reduce_max(out=mx[:], in_=ps[:], axis=AX.X)
-            nb = small.tile([P, 2], F32, tag="nb", name="nb")
-            nc.vector.tensor_scalar_mul(out=nb[:], in0=mx[:], scalar1=-10.0)
-            for t in range(2):
-                nc.scalar.activation(
-                    out=src_t[:, :, i, t, :],
-                    in_=ps[:, t, :].rearrange("p (q o) -> p q o", q=2),
-                    func=ACT.Exp,
-                    bias=nb[:, t:t + 1],
-                    scale=10.0,
-                    accum_out=sums[:, 2 * i + t:2 * i + t + 1],
-                )
-            nc.vector.reciprocal(out=rinv[:, 2 * i:2 * i + 2], in_=sums[:, 2 * i:2 * i + 2])
-            for t in range(2):
-                nc.vector.tensor_scalar_mul(
-                    out=src_t[:, :, i, t, :], in0=src_t[:, :, i, t, :], scalar1=rinv[:, 2 * i + t:2 * i + t + 1]
-                )
+        def prep_q(unit):
+            kind, a, b = unit
+            g = state[("g", unit)]
+            if kind == "L":
+                nc.vector.quantize_mx(out=lc_codes[:, a, :].bitcast(FP8X4), scales=lc_scales[:, a, :], in_=g[:])
+            else:
+                codes = mp.tile([P, 512], U32, tag="m_codes", name="m_codes", align_bytes=64)
+                scales = mp.tile([P, 512], U8, tag="m_scales", name="m_scales", align_bytes=64)
+                nc.vector.quantize_mx(out=codes[:].bitcast(FP8X4), scales=scales[:], in_=g[:])
+                state[("m", a, b)] = (codes, scales)
 
-        def centers(src_t, x, h, q):
+        def rd_mm(s):
+            h, k = divmod(s, 5)
+            codes, scales = state[("m", h, k)]
+            for x in range(2):
+                i = 2 * k + x
+                ps = scp.tile([P, 2, 256], F32, tag="ps", name="ps")
+                for t in range(2):
+                    c0 = ((1 - t) * 2 + x) * P
+                    nc.tensor.matmul_mx(
+                        out=ps[:, t, :],
+                        lhsT=codes[:, c0:c0 + P].bitcast(FP8X4),
+                        lhsT_scale=scales[:, c0:c0 + P],
+                        rhs=lc_codes[:, i, :].bitcast(FP8X4),
+                        rhs_scale=lc_scales[:, i, :],
+                        start=True,
+                        stop=True,
+                    )
+                state[("ps", s, x)] = ps
+
+        def rd_max(s):
+            for x in range(2):
+                ps = state[("ps", s, x)]
+                mx = small.tile([P, 2], F32, tag="mx", name="mx")
+                nc.vector.reduce_max(out=mx[:], in_=ps[:], axis=AX.X)
+                nb = small.tile([P, 2], F32, tag="nb", name="nb")
+                nc.vector.tensor_scalar_mul(out=nb[:], in0=mx[:], scalar1=-10.0)
+                state[("nb", s, x)] = nb
+
+        def rd_exp(s):
+            h, k = divmod(s, 5)
+            src_t, sums, rinv = state[("half", h)]
+            for x in range(2):
+                i = 2 * k + x
+                ps = state[("ps", s, x)]
+                nb = state[("nb", s, x)]
+                for t in range(2):
+                    nc.scalar.activation(
+                        out=src_t[:, :, i, t, :],
+                        in_=ps[:, t, :].rearrange("p (q o) -> p q o", q=2),
+                        func=ACT.Exp,
+                        bias=nb[:, t:t + 1],
+                        scale=10.0,
+                        accum_out=sums[:, 2 * i + t:2 * i + t + 1],
+                    )
+
+        def rd_norm(s):
+            h, k = divmod(s, 5)
+            src_t, sums, rinv = state[("half", h)]
+            nc.vector.reciprocal(out=rinv[:, 4 * k:4 * k + 4], in_=sums[:, 4 * k:4 * k + 4])
+            for j in range(4 * k, 4 * k + 4):
+                i, t = divmod(j, 2)
+                nc.vector.tensor_scalar_mul(out=src_t[:, :, i, t, :], in0=src_t[:, :, i, t, :], scalar1=rinv[:, j:j + 1])
+
+        def new_half(h):
+            src_t = srcp.tile([P, 2, NCHUNK, 3, P], F32, tag="src", name="src_t")
+            sums = stat.tile([P, 2 * NCHUNK], F32, tag="sums", name="sums")
+            rinv = stat.tile([P, 2 * NCHUNK], F32, tag="rinv", name="rinv")
+            state[("half", h)] = (src_t, sums, rinv)
+
+        def centers(x, h, q):
+            src_t = state[("half", h)][0]
             scv = sc_sb[(x, h)][:].rearrange("p (q o l) -> p q o l", q=2, l=30)
             nc.gpsimd.tensor_scalar(
                 out=src_t[:, q, :, 2, :].rearrange("p (g e) o -> p g o e", e=2),
@@ -138,7 +172,8 @@ def tile_contextualattention_t_kernel(tc, left, right, mid, sc00, sc01, sc10, sc
                 op1=ALU.add,
             )
 
-        def assemble(src_t, x, h, q):
+        def assemble(x, h, q):
+            src_t = state[("half", h)][0]
             o_t = slots.tile([P, 3840], F32, tag="slot", name="o_t")
             dst = o_t[:].rearrange("p (a e j) -> p a j e", e=RUN, j=30)
             srcv = src_t[:, q].rearrange("p i r (a e) -> p a (i r) e", e=RUN)
@@ -148,21 +183,63 @@ def tile_contextualattention_t_kernel(tc, left, right, mid, sc00, sc01, sc10, sc
                 out=outs[x][h * P:(h + 1) * P, q * P:(q + 1) * P, :].rearrange("b o j -> b (o j)"), in_=o_t[:]
             )
 
-        for h in range(2):
-            src_t = srcp.tile([P, 2, NCHUNK, 3, P], F32, tag="src", name="src_t")
-            sums = stat.tile([P, 2 * NCHUNK], F32, tag="sums", name="sums")
-            rinv = stat.tile([P, 2 * NCHUNK], F32, tag="rinv", name="rinv")
-            for k in range(5):
-                if h == 0:
-                    lc_unit(2 * k)
-                    lc_unit(2 * k + 1)
-                codes, scales = mid_unit(h, k)
-                scores(src_t, sums, rinv, 2 * k, codes, scales)
-                scores(src_t, sums, rinv, 2 * k + 1, codes, scales)
-            for q in range(2):
-                centers(src_t, 0, h, q)
-            for q in range(2):
-                assemble(src_t, 0, h, q)
-                centers(src_t, 1, h, q)
-            for q in range(2):
-                assemble(src_t, 1, h, q)
+        def lcu(i):
+            return ("L", i, 0)
+
+        def midu(h, k):
+            return ("M", h, k)
+
+        preps = [
+            [lcu(0), lcu(1), lcu(2), lcu(3), midu(0, 0)],
+            [lcu(4), midu(0, 1)],
+            [lcu(5), lcu(6), midu(0, 2)],
+            [lcu(7), lcu(8), midu(0, 3)],
+            [lcu(9), midu(0, 4)],
+        ] + [[midu(1, k)] for k in range(5)]
+
+        def do_prep(units):
+            for unit in units:
+                prep_t(unit)
+            for unit in units:
+                prep_e(unit)
+            for unit in units:
+                prep_q(unit)
+
+        new_half(0)
+        do_prep(preps[0])
+        for s in range(11):
+            if s < 10:
+                rd_mm(s)
+            nxt = preps[s + 1] if s + 1 < 10 else []
+            for unit in nxt:
+                prep_t(unit)
+            if s < 10:
+                rd_max(s)
+            if s == 4:
+                new_half(1)
+            if s >= 1:
+                rd_exp(s - 1)
+                rd_norm(s - 1)
+            for unit in nxt:
+                prep_e(unit)
+            for unit in nxt:
+                prep_q(unit)
+            if s == 2:
+                centers(0, 0, 0)
+                centers(0, 0, 1)
+            if s == 4:
+                centers(0, 1, 0)
+                centers(0, 1, 1)
+            if s == 5:
+                for q in range(2):
+                    assemble(0, 0, q)
+                    centers(1, 0, q)
+            if s == 7:
+                assemble(1, 0, 0)
+            if s == 8:
+                assemble(1, 0, 1)
+        for q in range(2):
+            assemble(0, 1, q)
+            centers(1, 1, q)
+        for q in range(2):
+            assemble(1, 1, q)

@@ -163,13 +163,9 @@ def tile_contextualattention_t_kernel(tc, left, right, mid, sc00, sc01, sc10, sc
         def centers(x, h, q):
             src_t = state[("half", h)][0]
             scv = sc_sb[(x, h)][:].rearrange("p (q o l) -> p q o l", q=2, l=30)
-            nc.gpsimd.tensor_scalar(
+            nc.vector.tensor_copy(
                 out=src_t[:, q, :, 2, :].rearrange("p (g e) o -> p g o e", e=2),
-                in0=scv[:, q, :, 0:10].rearrange("p o (g e) -> p g o e", e=2),
-                scalar1=1.0,
-                scalar2=0.0,
-                op0=ALU.mult,
-                op1=ALU.add,
+                in_=scv[:, q, :, 0:10].rearrange("p o (g e) -> p g o e", e=2),
             )
 
         def assemble(x, h, q):
@@ -197,49 +193,47 @@ def tile_contextualattention_t_kernel(tc, left, right, mid, sc00, sc01, sc10, sc
             [lcu(9), midu(0, 4)],
         ] + [[midu(1, k)] for k in range(5)]
 
-        def do_prep(units):
-            for unit in units:
-                prep_t(unit)
-            for unit in units:
-                prep_e(unit)
-            for unit in units:
-                prep_q(unit)
+        def rounds(s):
+            return 0 <= s < 10
 
         new_half(0)
-        do_prep(preps[0])
-        for s in range(11):
-            if s < 10:
-                rd_mm(s)
-            nxt = preps[s + 1] if s + 1 < 10 else []
-            for unit in nxt:
-                prep_t(unit)
-            if s < 10:
-                rd_max(s)
+        for s in range(-3, 11):
+            if rounds(s + 1):
+                rd_mm(s + 1)
+            if rounds(s + 3):
+                for unit in preps[s + 3]:
+                    prep_t(unit)
+            if rounds(s + 2):
+                for unit in preps[s + 2]:
+                    prep_e(unit)
             if s == 4:
                 new_half(1)
-            if s >= 1:
-                rd_exp(s - 1)
+            if rounds(s):
+                rd_max(s)
+                rd_exp(s)
+            if rounds(s - 1):
                 rd_norm(s - 1)
-            for unit in nxt:
-                prep_e(unit)
-            for unit in nxt:
-                prep_q(unit)
-            if s == 2:
+            if rounds(s + 2):
+                for unit in preps[s + 2]:
+                    prep_q(unit)
+            if s == 4:
                 centers(0, 0, 0)
                 centers(0, 0, 1)
-            if s == 4:
-                centers(0, 1, 0)
-                centers(0, 1, 1)
             if s == 5:
-                for q in range(2):
-                    assemble(0, 0, q)
-                    centers(1, 0, q)
+                assemble(0, 0, 0)
+                assemble(0, 0, 1)
+            if s == 6:
+                centers(1, 0, 0)
+                centers(1, 0, 1)
             if s == 7:
                 assemble(1, 0, 0)
+                centers(0, 1, 0)
             if s == 8:
                 assemble(1, 0, 1)
-        for q in range(2):
-            assemble(0, 1, q)
-            centers(1, 1, q)
-        for q in range(2):
-            assemble(1, 1, q)
+                centers(0, 1, 1)
+        assemble(0, 1, 0)
+        assemble(0, 1, 1)
+        centers(1, 1, 0)
+        assemble(1, 1, 0)
+        centers(1, 1, 1)
+        assemble(1, 1, 1)

@@ -18,7 +18,10 @@ FLOPS = 2 * 5120 * 256 * 512
 BYTES = 2 * 256 * 256 * 30 * 4 + 2 * 256 * 256 * 20 * 2 + 2 * 256 * 256 * 10 * 2
 
 RUN = 4
-V_GROUPS = 22
+NQ = 4
+QO = 64
+V_EXITS = (0, 2, 4)
+V_GROUPS = 10
 
 
 def tile_contextualattention_t_kernel(tc, left, right, mid, sc00, sc01, sc10, sc11, out_0, out_1):
@@ -80,8 +83,9 @@ def tile_contextualattention_t_kernel(tc, left, right, mid, sc00, sc01, sc10, sc
             kind, a, b = unit
             xt = state[("xt", unit)]
             if kind == "L":
-                g = gp.tile([P, 1024], BF16, tag="g_lc", name="g_lc", align_bytes=64)
-                nc.scalar.copy(out=g[:].bitcast(F32).rearrange("p (o u) -> p o u", u=2), in_=xt[:].rearrange("p u o -> p o u"))
+                g = gp.tile([P, 1024], BF16, tag="g_lc", name="g_lc", align_bytes=64, bufs=4)
+                eng_copy = nc.vector.tensor_copy if a in V_EXITS else nc.scalar.copy
+                eng_copy(out=g[:].bitcast(F32).rearrange("p (o u) -> p o u", u=2), in_=xt[:].rearrange("p u o -> p o u"))
             else:
                 g = gp.tile([P, 2048], BF16, tag="g_mid", name="g_mid", align_bytes=64)
                 gw = g[:].bitcast(F32).rearrange("p (v x b u) -> p v x b u", v=2, x=2, u=2)
@@ -121,62 +125,86 @@ def tile_contextualattention_t_kernel(tc, left, right, mid, sc00, sc01, sc10, sc
                 state[("ps", s, x)] = ps
 
         def rd_max(s):
+            mx = small.tile([P, 4], F32, tag="mx", name="mx")
             for x in range(2):
-                ps = state[("ps", s, x)]
-                mx = small.tile([P, 2], F32, tag="mx", name="mx")
-                nc.vector.reduce_max(out=mx[:], in_=ps[:], axis=AX.X)
-                nb = small.tile([P, 2], F32, tag="nb", name="nb")
-                nc.vector.tensor_scalar_mul(out=nb[:], in0=mx[:], scalar1=-10.0)
-                state[("nb", s, x)] = nb
+                nc.vector.reduce_max(out=mx[:, 2 * x:2 * x + 2], in_=state[("ps", s, x)][:], axis=AX.X)
+            nb = small.tile([P, 4], F32, tag="nb", name="nb")
+            nc.vector.tensor_scalar_mul(out=nb[:], in0=mx[:], scalar1=-10.0)
+            state[("nb", s)] = nb
 
-        def rd_exp(s):
+        def last_round(s):
             h, k = divmod(s, 5)
             src_t, sums, rinv = state[("half", h)]
+            mx = small.tile([P, 4], F32, tag="mx", name="mx")
+            nb = small.tile([P, 4], F32, tag="nb", name="nb")
+            state[("nb", s)] = nb
             for x in range(2):
+                c = slice(2 * x, 2 * x + 2)
+                nc.vector.reduce_max(out=mx[:, c], in_=state[("ps", s, x)][:], axis=AX.X)
+                nc.vector.tensor_scalar_mul(out=nb[:, c], in0=mx[:, c], scalar1=-10.0)
+                rd_exp(s, (x,))
+            for x in range(2):
+                j0 = 4 * k + 2 * x
+                nc.vector.reciprocal(out=rinv[:, j0:j0 + 2], in_=sums[:, j0:j0 + 2])
+                for j in range(j0, j0 + 2):
+                    norm(h, j, 0, 1)
+
+        def rd_exp(s, banks=(0, 1)):
+            h, k = divmod(s, 5)
+            src_t, sums, rinv = state[("half", h)]
+            for x in banks:
                 i = 2 * k + x
                 ps = state[("ps", s, x)]
-                nb = state[("nb", s, x)]
+                nb = state[("nb", s)]
                 for t in range(2):
                     nc.scalar.activation(
                         out=src_t[:, :, i, t, :],
-                        in_=ps[:, t, :].rearrange("p (q o) -> p q o", q=2),
+                        in_=ps[:, t, :].rearrange("p (q o) -> p q o", q=NQ),
                         func=ACT.Exp,
-                        bias=nb[:, t:t + 1],
+                        bias=nb[:, 2 * x + t:2 * x + t + 1],
                         scale=10.0,
                         accum_out=sums[:, 2 * i + t:2 * i + t + 1],
                     )
+
+        def norm(h, j, q0, q1):
+            src_t, sums, rinv = state[("half", h)]
+            i, t = divmod(j, 2)
+            nc.vector.tensor_scalar_mul(
+                out=src_t[:, q0:q1, i, t, :], in0=src_t[:, q0:q1, i, t, :], scalar1=rinv[:, j:j + 1]
+            )
 
         def rd_norm(s):
             h, k = divmod(s, 5)
             src_t, sums, rinv = state[("half", h)]
             nc.vector.reciprocal(out=rinv[:, 4 * k:4 * k + 4], in_=sums[:, 4 * k:4 * k + 4])
             for j in range(4 * k, 4 * k + 4):
-                i, t = divmod(j, 2)
-                nc.vector.tensor_scalar_mul(out=src_t[:, :, i, t, :], in0=src_t[:, :, i, t, :], scalar1=rinv[:, j:j + 1])
+                norm(h, j, 0, NQ if h == 0 else 1)
 
         def new_half(h):
-            src_t = srcp.tile([P, 2, NCHUNK, 3, P], F32, tag="src", name="src_t")
+            src_t = srcp.tile([P, NQ, NCHUNK, 3, QO], F32, tag="src", name="src_t")
             sums = stat.tile([P, 2 * NCHUNK], F32, tag="sums", name="sums")
             rinv = stat.tile([P, 2 * NCHUNK], F32, tag="rinv", name="rinv")
             state[("half", h)] = (src_t, sums, rinv)
 
-        def centers(x, h, q):
+        def centers(x, h, q, on_scalar=False):
             src_t = state[("half", h)][0]
-            scv = sc_sb[(x, h)][:].rearrange("p (q o l) -> p q o l", q=2, l=30)
-            nc.vector.tensor_copy(
+            eng_copy = nc.scalar.copy if on_scalar else nc.vector.tensor_copy
+            scv = sc_sb[(x, h)][:].rearrange("p (q o l) -> p q o l", q=NQ, l=30)
+            eng_copy(
                 out=src_t[:, q, :, 2, :].rearrange("p (g e) o -> p g o e", e=2),
                 in_=scv[:, q, :, 0:10].rearrange("p o (g e) -> p g o e", e=2),
             )
 
-        def assemble(x, h, q):
+        def assemble(x, h, q0, q1):
             src_t = state[("half", h)][0]
-            o_t = slots.tile([P, 3840], F32, tag="slot", name="o_t")
-            dst = o_t[:].rearrange("p (a e j) -> p a j e", e=RUN, j=30)
-            srcv = src_t[:, q].rearrange("p i r (a e) -> p a (i r) e", e=RUN)
-            nc.vector.tensor_copy(out=dst[:, 0:V_GROUPS], in_=srcv[:, 0:V_GROUPS])
-            nc.scalar.copy(out=dst[:, V_GROUPS:], in_=srcv[:, V_GROUPS:])
+            o_t = slots.tile([P, (q1 - q0) * QO * 30], F32, tag="slot", name="o_t")
+            dst = o_t[:].rearrange("p (q a e j) -> p q a j e", q=q1 - q0, e=RUN, j=30)
+            for q in range(q0, q1):
+                srcv = src_t[:, q].rearrange("p i r (a e) -> p a (i r) e", e=RUN)
+                nc.vector.tensor_copy(out=dst[:, q - q0, 0:V_GROUPS], in_=srcv[:, 0:V_GROUPS])
+                nc.scalar.copy(out=dst[:, q - q0, V_GROUPS:], in_=srcv[:, V_GROUPS:])
             nc.sync.dma_start(
-                out=outs[x][h * P:(h + 1) * P, q * P:(q + 1) * P, :].rearrange("b o j -> b (o j)"), in_=o_t[:]
+                out=outs[x][h * P:(h + 1) * P, q0 * QO:q1 * QO, :].rearrange("b o j -> b (o j)"), in_=o_t[:]
             )
 
         def lcu(i):
@@ -197,7 +225,7 @@ def tile_contextualattention_t_kernel(tc, left, right, mid, sc00, sc01, sc10, sc
             return 0 <= s < 10
 
         new_half(0)
-        for s in range(-3, 11):
+        for s in range(-3, 10):
             if rounds(s + 1):
                 rd_mm(s + 1)
             if rounds(s + 3):
@@ -208,32 +236,41 @@ def tile_contextualattention_t_kernel(tc, left, right, mid, sc00, sc01, sc10, sc
                     prep_e(unit)
             if s == 4:
                 new_half(1)
-            if rounds(s):
+            if rounds(s - 1) and s - 1 < 9:
+                early_norm = s == 9
+                if early_norm:
+                    rd_norm(s - 1)
+            if rounds(s) and s < 9:
                 rd_max(s)
                 rd_exp(s)
-            if rounds(s - 1):
+            if s == 9:
+                last_round(s)
+            if rounds(s - 1) and s < 9:
                 rd_norm(s - 1)
             if rounds(s + 2):
                 for unit in preps[s + 2]:
                     prep_q(unit)
             if s == 4:
-                centers(0, 0, 0)
-                centers(0, 0, 1)
+                for q in range(NQ):
+                    centers(0, 0, q)
             if s == 5:
-                assemble(0, 0, 0)
-                assemble(0, 0, 1)
+                assemble(0, 0, 0, 2)
+                assemble(0, 0, 2, 4)
             if s == 6:
-                centers(1, 0, 0)
-                centers(1, 0, 1)
+                for q in range(NQ):
+                    centers(1, 0, q, on_scalar=q < 2)
             if s == 7:
-                assemble(1, 0, 0)
-                centers(0, 1, 0)
+                assemble(1, 0, 0, 2)
             if s == 8:
-                assemble(1, 0, 1)
-                centers(0, 1, 1)
-        assemble(0, 1, 0)
-        assemble(0, 1, 1)
-        centers(1, 1, 0)
-        assemble(1, 1, 0)
-        centers(1, 1, 1)
-        assemble(1, 1, 1)
+                assemble(1, 0, 2, 4)
+                centers(0, 1, 0)
+        for q0, q1 in ((0, 1), (1, 2), (2, 4)):
+            if q0 > 0:
+                for j in range(2 * NCHUNK):
+                    norm(1, j, q0, q1)
+                for q in range(q0, q1):
+                    centers(0, 1, q)
+            assemble(0, 1, q0, q1)
+            for q in range(q0, q1):
+                centers(1, 1, q)
+            assemble(1, 1, q0, q1)

@@ -39,7 +39,6 @@ def tile_contextualattention_t_kernel(tc, left, right, mid, sc00, sc01, sc10, sc
         stat = ctx.enter_context(tc.tile_pool(name="stat", bufs=2))
         xtp = ctx.enter_context(tc.psum_pool(name="xtp", bufs=4))
         scp = ctx.enter_context(tc.psum_pool(name="scp", bufs=4))
-        ctx.enter_context(tc.manual_schedule())
 
         ident = const.tile([P, P], F32, name="ident")
         make_identity(nc, ident[:])

@@ -21,7 +21,7 @@ RUN = 4
 NQ = 4
 QO = 64
 V_EXITS = (0, 2, 4)
-V_GROUPS = 10
+V_GROUPS = (6, 4)
 
 
 def tile_contextualattention_t_kernel(tc, left, right, mid, sc00, sc01, sc10, sc11, out_0, out_1):
@@ -42,6 +42,11 @@ def tile_contextualattention_t_kernel(tc, left, right, mid, sc00, sc01, sc10, sc
 
         ident = const.tile([P, P], F32, name="ident")
         make_identity(nc, ident[:])
+        perm = const.tile([P, P], F32, name="perm")
+        nc.vector.tensor_copy(
+            out=perm[:].rearrange("p (a par e) -> p a par e", par=2, e=RUN),
+            in_=ident[:].rearrange("p (a e par) -> p a par e", par=2, e=RUN),
+        )
 
         left_sb = ins.tile([P, 2, 2560], BF16, name="left_sb")
         right_sb = ins.tile([P, 2, 2560], BF16, name="right_sb")
@@ -69,7 +74,7 @@ def tile_contextualattention_t_kernel(tc, left, right, mid, sc00, sc01, sc10, sc
                 xt = xtp.tile([P, 2, 256], F32, tag="xt", name="xt_lc")
                 for u in range(2):
                     for q in range(2):
-                        nc.tensor.transpose(out=xt[:, u, q * P:(q + 1) * P], in_=words[:, q, :, u, a % 5], identity=ident[:])
+                        nc.tensor.transpose(out=xt[:, u, q * P:(q + 1) * P], in_=words[:, q, :, u, a % 5], identity=perm[:])
             else:
                 words = mid_sb[a][:].bitcast(F32).rearrange("p (m u i) -> p m u i", u=2, i=10)
                 xt = xtp.tile([P, 2, 2, P], F32, tag="xt", name="xt_mid")
@@ -185,23 +190,23 @@ def tile_contextualattention_t_kernel(tc, left, right, mid, sc00, sc01, sc10, sc
             rinv = stat.tile([P, 2 * NCHUNK], F32, tag="rinv", name="rinv")
             state[("half", h)] = (src_t, sums, rinv)
 
-        def centers(x, h, q, on_scalar=False):
+        def centers(x, h, q):
             src_t = state[("half", h)][0]
-            eng_copy = nc.scalar.copy if on_scalar else nc.vector.tensor_copy
             scv = sc_sb[(x, h)][:].rearrange("p (q o l) -> p q o l", q=NQ, l=30)
-            eng_copy(
-                out=src_t[:, q, :, 2, :].rearrange("p (g e) o -> p g o e", e=2),
-                in_=scv[:, q, :, 0:10].rearrange("p o (g e) -> p g o e", e=2),
-            )
+            dst = src_t[:, q, :, 2, :].rearrange("p (g e2) (a par e) -> p par g a e e2", e2=2, par=2, e=RUN)
+            srcv = scv[:, q, :, 0:10].rearrange("p (a e par) (g e2) -> p par g a e e2", e2=2, par=2, e=RUN)
+            for par in range(2):
+                nc.vector.tensor_copy(out=dst[:, par], in_=srcv[:, par])
 
         def assemble(x, h, q0, q1):
             src_t = state[("half", h)][0]
             o_t = slots.tile([P, (q1 - q0) * QO * 30], F32, tag="slot", name="o_t")
-            dst = o_t[:].rearrange("p (q a e j) -> p q a j e", q=q1 - q0, e=RUN, j=30)
+            dst = o_t[:].rearrange("p (q a e par j) -> p q a par j e", q=q1 - q0, e=RUN, par=2, j=30)
             for q in range(q0, q1):
-                srcv = src_t[:, q].rearrange("p i r (a e) -> p a (i r) e", e=RUN)
-                nc.vector.tensor_copy(out=dst[:, q - q0, 0:V_GROUPS], in_=srcv[:, 0:V_GROUPS])
-                nc.scalar.copy(out=dst[:, q - q0, V_GROUPS:], in_=srcv[:, V_GROUPS:])
+                va = V_GROUPS[q % 2]
+                srcv = src_t[:, q].rearrange("p i r (a par e) -> p a par (i r) e", par=2, e=RUN)
+                nc.vector.tensor_copy(out=dst[:, q - q0, 0:va], in_=srcv[:, 0:va])
+                nc.scalar.copy(out=dst[:, q - q0, va:], in_=srcv[:, va:])
             nc.sync.dma_start(
                 out=outs[x][h * P:(h + 1) * P, q0 * QO:q1 * QO, :].rearrange("b o j -> b (o j)"), in_=o_t[:]
             )
@@ -257,7 +262,7 @@ def tile_contextualattention_t_kernel(tc, left, right, mid, sc00, sc01, sc10, sc
                 assemble(0, 0, 2, 4)
             if s == 6:
                 for q in range(NQ):
-                    centers(1, 0, q, on_scalar=q < 2)
+                    centers(1, 0, q)
             if s == 7:
                 assemble(1, 0, 0, 2)
             if s == 8:

@@ -21,7 +21,7 @@ RUN = 4
 NQ = 4
 QO = 64
 V_EXITS = (0, 2, 4)
-V_GROUPS = (6, 4)
+V_GROUPS = 10
 
 
 def tile_contextualattention_t_kernel(tc, left, right, mid, sc00, sc01, sc10, sc11, out_0, out_1):
@@ -42,11 +42,6 @@ def tile_contextualattention_t_kernel(tc, left, right, mid, sc00, sc01, sc10, sc
 
         ident = const.tile([P, P], F32, name="ident")
         make_identity(nc, ident[:])
-        perm = const.tile([P, P], F32, name="perm")
-        nc.vector.tensor_copy(
-            out=perm[:].rearrange("p (a par e) -> p a par e", par=2, e=RUN),
-            in_=ident[:].rearrange("p (a e par) -> p a par e", par=2, e=RUN),
-        )
 
         left_sb = ins.tile([P, 2, 2560], BF16, name="left_sb")
         right_sb = ins.tile([P, 2, 2560], BF16, name="right_sb")
@@ -74,7 +69,7 @@ def tile_contextualattention_t_kernel(tc, left, right, mid, sc00, sc01, sc10, sc
                 xt = xtp.tile([P, 2, 256], F32, tag="xt", name="xt_lc")
                 for u in range(2):
                     for q in range(2):
-                        nc.tensor.transpose(out=xt[:, u, q * P:(q + 1) * P], in_=words[:, q, :, u, a % 5], identity=perm[:])
+                        nc.tensor.transpose(out=xt[:, u, q * P:(q + 1) * P], in_=words[:, q, :, u, a % 5], identity=ident[:])
             else:
                 words = mid_sb[a][:].bitcast(F32).rearrange("p (m u i) -> p m u i", u=2, i=10)
                 xt = xtp.tile([P, 2, 2, P], F32, tag="xt", name="xt_mid")
@@ -182,7 +177,7 @@ def tile_contextualattention_t_kernel(tc, left, right, mid, sc00, sc01, sc10, sc
             src_t, sums, rinv = state[("half", h)]
             nc.vector.reciprocal(out=rinv[:, 4 * k:4 * k + 4], in_=sums[:, 4 * k:4 * k + 4])
             for j in range(4 * k, 4 * k + 4):
-                norm(h, j, 0, NQ if h == 0 else 1)
+                norm(h, j, 0, 1)
 
         def new_half(h):
             src_t = srcp.tile([P, NQ, NCHUNK, 3, QO], F32, tag="src", name="src_t")
@@ -190,23 +185,23 @@ def tile_contextualattention_t_kernel(tc, left, right, mid, sc00, sc01, sc10, sc
             rinv = stat.tile([P, 2 * NCHUNK], F32, tag="rinv", name="rinv")
             state[("half", h)] = (src_t, sums, rinv)
 
-        def centers(x, h, q):
+        def centers(x, h, q, on_scalar=False):
             src_t = state[("half", h)][0]
+            eng_copy = nc.scalar.copy if on_scalar else nc.vector.tensor_copy
             scv = sc_sb[(x, h)][:].rearrange("p (q o l) -> p q o l", q=NQ, l=30)
-            dst = src_t[:, q, :, 2, :].rearrange("p (g e2) (a par e) -> p par g a e e2", e2=2, par=2, e=RUN)
-            srcv = scv[:, q, :, 0:10].rearrange("p (a e par) (g e2) -> p par g a e e2", e2=2, par=2, e=RUN)
-            for par in range(2):
-                nc.vector.tensor_copy(out=dst[:, par], in_=srcv[:, par])
+            eng_copy(
+                out=src_t[:, q, :, 2, :].rearrange("p (g e) o -> p g o e", e=2),
+                in_=scv[:, q, :, 0:10].rearrange("p o (g e) -> p g o e", e=2),
+            )
 
         def assemble(x, h, q0, q1):
             src_t = state[("half", h)][0]
             o_t = slots.tile([P, (q1 - q0) * QO * 30], F32, tag="slot", name="o_t")
-            dst = o_t[:].rearrange("p (q a e par j) -> p q a par j e", q=q1 - q0, e=RUN, par=2, j=30)
+            dst = o_t[:].rearrange("p (q a e j) -> p q a j e", q=q1 - q0, e=RUN, j=30)
             for q in range(q0, q1):
-                va = V_GROUPS[q % 2]
-                srcv = src_t[:, q].rearrange("p i r (a par e) -> p a par (i r) e", par=2, e=RUN)
-                nc.vector.tensor_copy(out=dst[:, q - q0, 0:va], in_=srcv[:, 0:va])
-                nc.scalar.copy(out=dst[:, q - q0, va:], in_=srcv[:, va:])
+                srcv = src_t[:, q].rearrange("p i r (a e) -> p a (i r) e", e=RUN)
+                nc.vector.tensor_copy(out=dst[:, q - q0, 0:V_GROUPS], in_=srcv[:, 0:V_GROUPS])
+                nc.scalar.copy(out=dst[:, q - q0, V_GROUPS:], in_=srcv[:, V_GROUPS:])
             nc.sync.dma_start(
                 out=outs[x][h * P:(h + 1) * P, q0 * QO:q1 * QO, :].rearrange("b o j -> b (o j)"), in_=o_t[:]
             )
@@ -224,6 +219,18 @@ def tile_contextualattention_t_kernel(tc, left, right, mid, sc00, sc01, sc10, sc
             [lcu(7), lcu(8), midu(0, 3)],
             [lcu(9), midu(0, 4)],
         ] + [[midu(1, k)] for k in range(5)]
+
+        def stages(h):
+            for q0, q1 in ((0, 1), (1, 2), (2, 4)):
+                if q0 > 0:
+                    for j in range(2 * NCHUNK):
+                        norm(h, j, q0, q1)
+                    for q in range(q0, q1):
+                        centers(0, h, q)
+                assemble(0, h, q0, q1)
+                for q in range(q0, q1):
+                    centers(1, h, q)
+                assemble(1, h, q0, q1)
 
         def rounds(s):
             return 0 <= s < 10
@@ -255,26 +262,9 @@ def tile_contextualattention_t_kernel(tc, left, right, mid, sc00, sc01, sc10, sc
                 for unit in preps[s + 2]:
                     prep_q(unit)
             if s == 4:
-                for q in range(NQ):
-                    centers(0, 0, q)
+                centers(0, 0, 0)
             if s == 5:
-                assemble(0, 0, 0, 2)
-                assemble(0, 0, 2, 4)
-            if s == 6:
-                for q in range(NQ):
-                    centers(1, 0, q)
-            if s == 7:
-                assemble(1, 0, 0, 2)
+                stages(0)
             if s == 8:
-                assemble(1, 0, 2, 4)
                 centers(0, 1, 0)
-        for q0, q1 in ((0, 1), (1, 2), (2, 4)):
-            if q0 > 0:
-                for j in range(2 * NCHUNK):
-                    norm(1, j, q0, q1)
-                for q in range(q0, q1):
-                    centers(0, 1, q)
-            assemble(0, 1, q0, q1)
-            for q in range(q0, q1):
-                centers(1, 1, q)
-            assemble(1, 1, q0, q1)
+        stages(1)

@@ -29,7 +29,7 @@ def tile_contextualattention_t_kernel(tc, left, right, mid, sc00, sc01, sc10, sc
     outs = (out_0, out_1)
     with ExitStack() as ctx:
         const = ctx.enter_context(tc.tile_pool(name="const", bufs=1))
-        ins = ctx.enter_context(tc.tile_pool(name="ins", bufs=1))
+        ins = ctx.enter_context(tc.tile_pool(name="ins", bufs=4))
         slots = ctx.enter_context(tc.tile_pool(name="slots", bufs=6))
         srcp = ctx.enter_context(tc.tile_pool(name="srcp", bufs=2))
         keep = ctx.enter_context(tc.tile_pool(name="keep", bufs=1))
@@ -43,9 +43,9 @@ def tile_contextualattention_t_kernel(tc, left, right, mid, sc00, sc01, sc10, sc
         ident = const.tile([P, P], F32, name="ident")
         make_identity(nc, ident[:])
 
-        left_sb = ins.tile([P, 2, 2560], BF16, name="left_sb")
-        right_sb = ins.tile([P, 2, 2560], BF16, name="right_sb")
-        mid_sb = [ins.tile([P, 5120], BF16, name="mid_sb%d" % h) for h in range(2)]
+        left_sb = ins.tile([P, 2, 2560], BF16, tag="in10", name="left_sb")
+        right_sb = ins.tile([P, 2, 2560], BF16, tag="in10", name="right_sb")
+        mid_sb = [ins.tile([P, 5120], BF16, tag="in10", name="mid_sb%d" % h) for h in range(2)]
         nc.sync.dma_start(out=left_sb[:], in_=left.rearrange("(q o) c l -> o q (c l)", q=2))
         nc.sync.dma_start(out=mid_sb[0][:], in_=mid[0:P].rearrange("b c l -> b (c l)"))
         nc.sync.dma_start(out=right_sb[:], in_=right.rearrange("(q o) c l -> o q (c l)", q=2))
@@ -196,7 +196,10 @@ def tile_contextualattention_t_kernel(tc, left, right, mid, sc00, sc01, sc10, sc
 
         def assemble(x, h, q0, q1):
             src_t = state[("half", h)][0]
-            o_t = slots.tile([P, (q1 - q0) * QO * 30], F32, tag="slot", name="o_t")
+            if q1 - q0 == 1:
+                o_t = ins.tile([P, QO * 30], F32, tag="in10", name="o_s")
+            else:
+                o_t = slots.tile([P, (q1 - q0) * QO * 30], F32, tag="slot", name="o_t")
             dst = o_t[:].rearrange("p (q a e j) -> p q a j e", q=q1 - q0, e=RUN, j=30)
             for q in range(q0, q1):
                 srcv = src_t[:, q].rearrange("p i r (a e) -> p a (i r) e", e=RUN)

@@ -9,7 +9,6 @@ U32 = mybir.dt.uint32
 U8 = mybir.dt.uint8
 FP8X4 = mybir.dt.float8_e4m3fn_x4
 ACT = mybir.ActivationFunctionType
-ALU = mybir.AluOpType
 AX = mybir.AxisListType
 
 P = 128
@@ -17,11 +16,11 @@ NCHUNK = 10
 FLOPS = 2 * 5120 * 256 * 512
 BYTES = 2 * 256 * 256 * 30 * 4 + 2 * 256 * 256 * 20 * 2 + 2 * 256 * 256 * 10 * 2
 
-RUN = 4
+RUN = 2
 NQ = 4
 QO = 64
-V_EXITS = (0, 2, 4)
-V_GROUPS = 10
+V_EXITS = (1, 3)
+V_GROUPS = 6
 
 
 def tile_contextualattention_t_kernel(tc, left, right, mid, sc00, sc01, sc10, sc11, out_0, out_1):
@@ -30,7 +29,7 @@ def tile_contextualattention_t_kernel(tc, left, right, mid, sc00, sc01, sc10, sc
     with ExitStack() as ctx:
         const = ctx.enter_context(tc.tile_pool(name="const", bufs=1))
         ins = ctx.enter_context(tc.tile_pool(name="ins", bufs=4))
-        slots = ctx.enter_context(tc.tile_pool(name="slots", bufs=6))
+        slots = ctx.enter_context(tc.tile_pool(name="slots", bufs=4))
         srcp = ctx.enter_context(tc.tile_pool(name="srcp", bufs=2))
         keep = ctx.enter_context(tc.tile_pool(name="keep", bufs=1))
         gp = ctx.enter_context(tc.tile_pool(name="gp", bufs=2))
@@ -42,6 +41,7 @@ def tile_contextualattention_t_kernel(tc, left, right, mid, sc00, sc01, sc10, sc
 
         ident = const.tile([P, P], F32, name="ident")
         make_identity(nc, ident[:])
+        ctx.enter_context(tc.manual_schedule())
 
         left_sb = ins.tile([P, 2, 2560], BF16, tag="in10", name="left_sb")
         right_sb = ins.tile([P, 2, 2560], BF16, tag="in10", name="right_sb")
@@ -49,16 +49,24 @@ def tile_contextualattention_t_kernel(tc, left, right, mid, sc00, sc01, sc10, sc
         nc.sync.dma_start(out=left_sb[:], in_=left.rearrange("(q o) c l -> o q (c l)", q=2))
         nc.sync.dma_start(out=mid_sb[0][:], in_=mid[0:P].rearrange("b c l -> b (c l)"))
         nc.sync.dma_start(out=right_sb[:], in_=right.rearrange("(q o) c l -> o q (c l)", q=2))
-        nc.sync.dma_start(out=mid_sb[1][:], in_=mid[P:2 * P].rearrange("b c l -> b (c l)"))
         sc_sb = {}
-        for h in range(2):
-            for x, sc in enumerate((sc00, sc10)):
-                t = slots.tile([P, 7680], BF16, tag="slot", name="sc_sb%d%d" % (x, h))
-                nc.sync.dma_start(out=t[:], in_=sc[h * P:(h + 1) * P].rearrange("b c l -> b (c l)"))
-                sc_sb[(x, h)] = t
+
+        def load_sc(x, h):
+            t = slots.tile([P, 7680], BF16, tag="slot", name="sc_sb%d%d" % (x, h))
+            sc = (sc00, sc10)[x]
+            nc.sync.dma_start(out=t[:], in_=sc[h * P:(h + 1) * P].rearrange("b c l -> b (c l)"))
+            sc_sb[(x, h)] = t
+
+        load_sc(0, 0)
+        nc.sync.dma_start(out=mid_sb[1][:], in_=mid[P:2 * P].rearrange("b c l -> b (c l)"))
+        load_sc(1, 0)
+        load_sc(0, 1)
+        load_sc(1, 1)
 
         lc_codes = keep.tile([P, NCHUNK, 256], U32, name="lc_codes", align_bytes=64)
         lc_scales = keep.tile([P, NCHUNK, 256], U8, name="lc_scales", align_bytes=64)
+        zero_tap = keep.tile([P, 2 * 5, 256], U32, name="zero_tap", align_bytes=64)
+        nc.gpsimd.memset(zero_tap[:], 0)
         state = {}
 
         def prep_t(unit):
@@ -67,8 +75,8 @@ def tile_contextualattention_t_kernel(tc, left, right, mid, sc00, sc01, sc10, sc
                 sb = left_sb if a < 5 else right_sb
                 words = sb[:].bitcast(F32).rearrange("p q (m u i) -> p q m u i", u=2, i=5)
                 xt = xtp.tile([P, 2, 256], F32, tag="xt", name="xt_lc")
-                for u in range(2):
-                    for q in range(2):
+                for q in range(2):
+                    for u in range(2):
                         nc.tensor.transpose(out=xt[:, u, q * P:(q + 1) * P], in_=words[:, q, :, u, a % 5], identity=ident[:])
             else:
                 words = mid_sb[a][:].bitcast(F32).rearrange("p (m u i) -> p m u i", u=2, i=10)
@@ -86,11 +94,9 @@ def tile_contextualattention_t_kernel(tc, left, right, mid, sc00, sc01, sc10, sc
                 eng_copy = nc.vector.tensor_copy if a in V_EXITS else nc.scalar.copy
                 eng_copy(out=g[:].bitcast(F32).rearrange("p (o u) -> p o u", u=2), in_=xt[:].rearrange("p u o -> p o u"))
             else:
-                g = gp.tile([P, 2048], BF16, tag="g_mid", name="g_mid", align_bytes=64)
-                gw = g[:].bitcast(F32).rearrange("p (v x b u) -> p v x b u", v=2, x=2, u=2)
-                nc.scalar.copy(out=gw[:, 0], in_=xt[:].rearrange("p x u b -> p x b u"))
-                tap0 = xt[:].bitcast(BF16).rearrange("p x u (b e) -> p x b u e", e=2)[:, :, :, :, 0]
-                nc.scalar.copy(out=gw[:, 1], in_=tap0)
+                g = gp.tile([P, 1024], BF16, tag="g_mid", name="g_mid", align_bytes=64)
+                gw = g[:].bitcast(F32).rearrange("p (x b u) -> p x b u", x=2, u=2)
+                nc.scalar.copy(out=gw, in_=xt[:].rearrange("p x u b -> p x b u"))
             state[("g", unit)] = g
 
         def prep_q(unit):
@@ -99,85 +105,77 @@ def tile_contextualattention_t_kernel(tc, left, right, mid, sc00, sc01, sc10, sc
             if kind == "L":
                 nc.vector.quantize_mx(out=lc_codes[:, a, :].bitcast(FP8X4), scales=lc_scales[:, a, :], in_=g[:])
             else:
-                codes = mp.tile([P, 512], U32, tag="m_codes", name="m_codes", align_bytes=64)
-                scales = mp.tile([P, 512], U8, tag="m_scales", name="m_scales", align_bytes=64)
+                codes = mp.tile([P, 256], U32, tag="m_codes", name="m_codes", align_bytes=64)
+                scales = mp.tile([P, 256], U8, tag="m_scales", name="m_scales", align_bytes=64)
                 nc.vector.quantize_mx(out=codes[:].bitcast(FP8X4), scales=scales[:], in_=g[:])
                 state[("m", a, b)] = (codes, scales)
+
+        def prep_z(unit):
+            kind, a, b = unit
+            codes = state[("m", a, b)][0]
+            nc.vector.tensor_copy(
+                out=zero_tap[:, 5 * a + b, :].bitcast(U8).rearrange("p (n e) -> p n e", e=2)[:, :, 1],
+                in_=codes[:].bitcast(U8).rearrange("p (n e) -> p n e", e=2)[:, :, 0],
+            )
 
         def rd_mm(s):
             h, k = divmod(s, 5)
             codes, scales = state[("m", h, k)]
+            late = zero_tap[:, 5 * h + k, :]
             for x in range(2):
-                i = 2 * k + x
-                ps = scp.tile([P, 2, 256], F32, tag="ps", name="ps")
-                for t in range(2):
-                    c0 = ((1 - t) * 2 + x) * P
+                state[("ps", s, x)] = scp.tile([P, 2, 256], F32, tag="ps", name="ps")
+            for t, words in ((1, codes), (0, late)):
+                for x in range(2):
+                    i = 2 * k + x
                     nc.tensor.matmul_mx(
-                        out=ps[:, t, :],
-                        lhsT=codes[:, c0:c0 + P].bitcast(FP8X4),
-                        lhsT_scale=scales[:, c0:c0 + P],
+                        out=state[("ps", s, x)][:, t, :],
+                        lhsT=words[:, x * P:(x + 1) * P].bitcast(FP8X4),
+                        lhsT_scale=scales[:, x * P:(x + 1) * P],
                         rhs=lc_codes[:, i, :].bitcast(FP8X4),
                         rhs_scale=lc_scales[:, i, :],
                         start=True,
                         stop=True,
                     )
-                state[("ps", s, x)] = ps
 
-        def rd_max(s):
-            mx = small.tile([P, 4], F32, tag="mx", name="mx")
-            for x in range(2):
-                nc.vector.reduce_max(out=mx[:, 2 * x:2 * x + 2], in_=state[("ps", s, x)][:], axis=AX.X)
-            nb = small.tile([P, 4], F32, tag="nb", name="nb")
-            nc.vector.tensor_scalar_mul(out=nb[:], in0=mx[:], scalar1=-10.0)
-            state[("nb", s)] = nb
+        def rd_max(s, x):
+            mx = small.tile([P, 2], F32, tag="mx", name="mx")
+            nc.vector.reduce_max(out=mx[:], in_=state[("ps", s, x)][:], axis=AX.X)
+            state[("mx", s, x)] = mx
 
-        def last_round(s):
+        def rd_nb(s, x):
+            nb = small.tile([P, 2], F32, tag="nb", name="nb")
+            nc.vector.tensor_scalar_mul(out=nb[:], in0=state[("mx", s, x)][:], scalar1=-10.0)
+            state[("nb", s, x)] = nb
+
+        def rd_exp(s, x):
             h, k = divmod(s, 5)
             src_t, sums, rinv = state[("half", h)]
-            mx = small.tile([P, 4], F32, tag="mx", name="mx")
-            nb = small.tile([P, 4], F32, tag="nb", name="nb")
-            state[("nb", s)] = nb
-            for x in range(2):
-                c = slice(2 * x, 2 * x + 2)
-                nc.vector.reduce_max(out=mx[:, c], in_=state[("ps", s, x)][:], axis=AX.X)
-                nc.vector.tensor_scalar_mul(out=nb[:, c], in0=mx[:, c], scalar1=-10.0)
-                rd_exp(s, (x,))
-            for x in range(2):
-                j0 = 4 * k + 2 * x
-                nc.vector.reciprocal(out=rinv[:, j0:j0 + 2], in_=sums[:, j0:j0 + 2])
-                for j in range(j0, j0 + 2):
-                    norm(h, j, 0, 1)
+            nb = state[("nb", s, x)]
+            i = 2 * k + x
+            ps = state[("ps", s, x)]
+            for t in range(2):
+                nc.scalar.activation(
+                    out=src_t[:, :, i, t, :].rearrange("p q (y o) -> p q y o", y=2),
+                    in_=ps[:, t, :].rearrange("p (q o y) -> p q y o", q=NQ, y=2),
+                    func=ACT.Exp,
+                    bias=nb[:, t:t + 1],
+                    scale=10.0,
+                    accum_out=sums[:, 2 * i + t:2 * i + t + 1],
+                )
 
-        def rd_exp(s, banks=(0, 1)):
-            h, k = divmod(s, 5)
-            src_t, sums, rinv = state[("half", h)]
-            for x in banks:
-                i = 2 * k + x
-                ps = state[("ps", s, x)]
-                nb = state[("nb", s)]
-                for t in range(2):
-                    nc.scalar.activation(
-                        out=src_t[:, :, i, t, :],
-                        in_=ps[:, t, :].rearrange("p (q o) -> p q o", q=NQ),
-                        func=ACT.Exp,
-                        bias=nb[:, 2 * x + t:2 * x + t + 1],
-                        scale=10.0,
-                        accum_out=sums[:, 2 * i + t:2 * i + t + 1],
-                    )
-
-        def norm(h, j, q0, q1):
-            src_t, sums, rinv = state[("half", h)]
-            i, t = divmod(j, 2)
-            nc.vector.tensor_scalar_mul(
-                out=src_t[:, q0:q1, i, t, :], in0=src_t[:, q0:q1, i, t, :], scalar1=rinv[:, j:j + 1]
-            )
-
-        def rd_norm(s):
+        def rd_recip(s):
             h, k = divmod(s, 5)
             src_t, sums, rinv = state[("half", h)]
             nc.vector.reciprocal(out=rinv[:, 4 * k:4 * k + 4], in_=sums[:, 4 * k:4 * k + 4])
+
+        def rd_norm(s, q0, q1):
+            h, k = divmod(s, 5)
+            src_t, sums, rinv = state[("half", h)]
             for j in range(4 * k, 4 * k + 4):
-                norm(h, j, 0, 1)
+                i, t = divmod(j, 2)
+                nc.vector.tensor_scalar_mul(
+                    out=src_t[:, q0:q1, i, t, :], in0=src_t[:, q0:q1, i, t, :], scalar1=rinv[:, j:j + 1]
+                )
 
         def new_half(h):
             src_t = srcp.tile([P, NQ, NCHUNK, 3, QO], F32, tag="src", name="src_t")
@@ -185,89 +183,131 @@ def tile_contextualattention_t_kernel(tc, left, right, mid, sc00, sc01, sc10, sc
             rinv = stat.tile([P, 2 * NCHUNK], F32, tag="rinv", name="rinv")
             state[("half", h)] = (src_t, sums, rinv)
 
-        def centers(x, h, q, on_scalar=False):
+        def centers(x, h, q):
             src_t = state[("half", h)][0]
-            eng_copy = nc.scalar.copy if on_scalar else nc.vector.tensor_copy
-            scv = sc_sb[(x, h)][:].rearrange("p (q o l) -> p q o l", q=NQ, l=30)
-            eng_copy(
-                out=src_t[:, q, :, 2, :].rearrange("p (g e) o -> p g o e", e=2),
-                in_=scv[:, q, :, 0:10].rearrange("p o (g e) -> p g o e", e=2),
+            scv = sc_sb[(x, h)][:].rearrange("p (q o y l) -> p q y o l", q=NQ, y=2, l=30)
+            nc.vector.tensor_copy(
+                out=src_t[:, q, :, 2, :].rearrange("p (g e) (y o) -> p g y o e", e=2, y=2),
+                in_=scv[:, q, :, :, 0:10].rearrange("p y o (g e) -> p g y o e", e=2),
             )
+
+        def out_tile(n):
+            if n == 1:
+                return ins.tile([P, QO * 30], F32, tag="o_s", name="o_s")
+            return slots.tile([P, n * QO * 30], F32, tag="slot", name="o_t")
 
         def assemble(x, h, q0, q1):
             src_t = state[("half", h)][0]
-            if q1 - q0 == 1:
-                o_t = ins.tile([P, QO * 30], F32, tag="in10", name="o_s")
-            else:
-                o_t = slots.tile([P, (q1 - q0) * QO * 30], F32, tag="slot", name="o_t")
-            dst = o_t[:].rearrange("p (q a e j) -> p q a j e", q=q1 - q0, e=RUN, j=30)
+            o_t = out_tile(q1 - q0)
+            dst = o_t[:].rearrange("p (q a e y j) -> p q a y j e", q=q1 - q0, e=RUN, y=2, j=30)
             for q in range(q0, q1):
-                srcv = src_t[:, q].rearrange("p i r (a e) -> p a (i r) e", e=RUN)
+                srcv = src_t[:, q].rearrange("p i r (y a e) -> p a y (i r) e", y=2, e=RUN)
                 nc.vector.tensor_copy(out=dst[:, q - q0, 0:V_GROUPS], in_=srcv[:, 0:V_GROUPS])
                 nc.scalar.copy(out=dst[:, q - q0, V_GROUPS:], in_=srcv[:, V_GROUPS:])
             nc.sync.dma_start(
                 out=outs[x][h * P:(h + 1) * P, q0 * QO:q1 * QO, :].rearrange("b o j -> b (o j)"), in_=o_t[:]
             )
 
-        def lcu(i):
+        def L(i):
             return ("L", i, 0)
 
-        def midu(h, k):
+        def M(h, k):
             return ("M", h, k)
 
-        preps = [
-            [lcu(0), lcu(1), lcu(2), lcu(3), midu(0, 0)],
-            [lcu(4), midu(0, 1)],
-            [lcu(5), lcu(6), midu(0, 2)],
-            [lcu(7), lcu(8), midu(0, 3)],
-            [lcu(9), midu(0, 4)],
-        ] + [[midu(1, k)] for k in range(5)]
+        def T(*us):
+            for u in us:
+                prep_t(u)
 
-        def stages(h):
-            for q0, q1 in ((0, 1), (1, 2), (2, 4)):
-                if q0 > 0:
-                    for j in range(2 * NCHUNK):
-                        norm(h, j, q0, q1)
-                    for q in range(q0, q1):
-                        centers(0, h, q)
-                assemble(0, h, q0, q1)
-                for q in range(q0, q1):
-                    centers(1, h, q)
-                assemble(1, h, q0, q1)
+        def E(*us):
+            for u in us:
+                prep_e(u)
 
-        def rounds(s):
-            return 0 <= s < 10
+        def Q(*us):
+            for u in us:
+                prep_q(u)
 
         new_half(0)
-        for s in range(-3, 10):
-            if rounds(s + 1):
-                rd_mm(s + 1)
-            if rounds(s + 3):
-                for unit in preps[s + 3]:
-                    prep_t(unit)
-            if rounds(s + 2):
-                for unit in preps[s + 2]:
-                    prep_e(unit)
-            if s == 4:
-                new_half(1)
-            if rounds(s - 1) and s - 1 < 9:
-                early_norm = s == 9
-                if early_norm:
-                    rd_norm(s - 1)
-            if rounds(s) and s < 9:
-                rd_max(s)
-                rd_exp(s)
-            if s == 9:
-                last_round(s)
-            if rounds(s - 1) and s < 9:
-                rd_norm(s - 1)
-            if rounds(s + 2):
-                for unit in preps[s + 2]:
-                    prep_q(unit)
-            if s == 4:
-                centers(0, 0, 0)
-            if s == 5:
-                stages(0)
-            if s == 8:
-                centers(0, 1, 0)
-        stages(1)
+        new_half(1)
+
+        def LS(k):
+            return [L(2 * k), L(2 * k + 1)] if k < 5 else []
+
+        def MS(r):
+            return [M(r // 5, r % 5)] if r < 10 else []
+
+        def round_(r, early=(), late=()):
+            h = r // 5
+            ls = LS(r + 2)
+            E(*ls)
+            rd_max(r, 0)
+            Q(*MS(r + 1))
+            rd_nb(r, 0)
+            T(*MS(r + 2))
+            for f in early[:1]:
+                f()
+            rd_exp(r, 0)
+            rd_max(r, 1)
+            for u in MS(r + 1):
+                prep_z(u)
+            rd_nb(r, 1)
+            E(*MS(r + 2))
+            rd_exp(r, 1)
+            for f in early[1:]:
+                f()
+            Q(*ls)
+            if r < 9:
+                rd_mm(r + 1)
+            T(*LS(r + 3))
+            if r % 5 > 0:
+                rd_recip(r - 1)
+            for f in late:
+                f()
+            if r % 5 > 0:
+                rd_norm(r - 1, 0, 1 if h == 0 else 4)
+
+        def c(x, h, q):
+            return lambda: centers(x, h, q)
+
+        def a(x, h, q):
+            return lambda: assemble(x, h, q, q + 1)
+
+        def n(r, q0, q1):
+            return lambda: rd_norm(r, q0, q1)
+
+        T(*LS(0))
+        T(*MS(0))
+        E(*LS(0))
+        E(*MS(0))
+        T(*LS(1))
+        Q(*LS(0))
+        Q(*MS(0))
+        E(*LS(1))
+        prep_z(MS(0)[0])
+        T(*MS(1))
+        rd_mm(0)
+        E(*MS(1))
+        Q(*LS(1))
+        T(*LS(2))
+        for r in range(4):
+            round_(r)
+        round_(4, (), (c(0, 0, 0),))
+        rd_recip(4)
+        centers(0, 0, 1)
+        rd_norm(4, 0, 1)
+        centers(0, 0, 2)
+        assemble(0, 0, 0, 1)
+        for r in range(5):
+            rd_norm(r, 1, 4)
+        round_(5, (a(0, 0, 1),), (c(0, 0, 3), c(1, 0, 0), a(0, 0, 2)))
+        round_(6, (a(1, 0, 0),), (c(1, 0, 1), a(0, 0, 3), c(1, 0, 2)))
+        round_(7, (a(1, 0, 1),), (a(1, 0, 2), c(1, 0, 3)))
+        round_(8, (a(1, 0, 3),), (c(0, 1, 0), c(0, 1, 1)))
+        round_(9, (c(0, 1, 2),), (c(0, 1, 3),))
+        rd_recip(9)
+        rd_norm(9, 0, 4)
+        assemble(0, 1, 0, 1)
+        for q in range(4):
+            if q < 3:
+                assemble(0, 1, q + 1, q + 2)
+            centers(1, 1, q)
+            assemble(1, 1, q, q + 1)

@@ -20,7 +20,7 @@ RUN = 2
 NQ = 4
 QO = 64
 V_EXITS = (1, 3)
-V_GROUPS = 6
+V_GROUPS = 8
 
 
 def tile_contextualattention_t_kernel(tc, left, right, mid, sc00, sc01, sc10, sc11, out_0, out_1):
@@ -168,14 +168,16 @@ def tile_contextualattention_t_kernel(tc, left, right, mid, sc00, sc01, sc10, sc
             src_t, sums, rinv = state[("half", h)]
             nc.vector.reciprocal(out=rinv[:, 4 * k:4 * k + 4], in_=sums[:, 4 * k:4 * k + 4])
 
-        def rd_norm(s, q0, q1):
+        def rd_norm(s, q0, q1, on_scalar=()):
             h, k = divmod(s, 5)
             src_t, sums, rinv = state[("half", h)]
             for j in range(4 * k, 4 * k + 4):
                 i, t = divmod(j, 2)
-                nc.vector.tensor_scalar_mul(
-                    out=src_t[:, q0:q1, i, t, :], in0=src_t[:, q0:q1, i, t, :], scalar1=rinv[:, j:j + 1]
-                )
+                rows = src_t[:, q0:q1, i, t, :]
+                if j % 4 in on_scalar:
+                    nc.scalar.activation(out=rows, in_=rows, func=ACT.Copy, scale=rinv[:, j:j + 1])
+                else:
+                    nc.vector.tensor_scalar_mul(out=rows, in0=rows, scalar1=rinv[:, j:j + 1])
 
         def new_half(h):
             src_t = srcp.tile([P, NQ, NCHUNK, 3, QO], F32, tag="src", name="src_t")
@@ -183,10 +185,10 @@ def tile_contextualattention_t_kernel(tc, left, right, mid, sc00, sc01, sc10, sc
             rinv = stat.tile([P, 2 * NCHUNK], F32, tag="rinv", name="rinv")
             state[("half", h)] = (src_t, sums, rinv)
 
-        def centers(x, h, q):
+        def centers(x, h, q, copy=nc.vector.tensor_copy):
             src_t = state[("half", h)][0]
             scv = sc_sb[(x, h)][:].rearrange("p (q o y l) -> p q y o l", q=NQ, y=2, l=30)
-            nc.vector.tensor_copy(
+            copy(
                 out=src_t[:, q, :, 2, :].rearrange("p (g e) (y o) -> p g y o e", e=2, y=2),
                 in_=scv[:, q, :, :, 0:10].rearrange("p y o (g e) -> p g y o e", e=2),
             )
@@ -229,18 +231,19 @@ def tile_contextualattention_t_kernel(tc, left, right, mid, sc00, sc01, sc10, sc
         new_half(0)
         new_half(1)
 
-        def LS(k):
-            return [L(2 * k), L(2 * k + 1)] if k < 5 else []
+        def LS(r):
+            return [[L(5)], [L(6), L(7)], [L(8), L(9)]][r] if r < 3 else []
 
         def MS(r):
             return [M(r // 5, r % 5)] if r < 10 else []
 
         def round_(r, early=(), late=()):
-            h = r // 5
-            ls = LS(r + 2)
+            ls = LS(r)
             E(*ls)
             rd_max(r, 0)
             Q(*MS(r + 1))
+            if r == 9:
+                centers(0, 1, 0)
             rd_nb(r, 0)
             T(*MS(r + 2))
             for f in early[:1]:
@@ -249,6 +252,10 @@ def tile_contextualattention_t_kernel(tc, left, right, mid, sc00, sc01, sc10, sc
             rd_max(r, 1)
             for u in MS(r + 1):
                 prep_z(u)
+            if r == 9:
+                centers(0, 1, 1)
+            if r % 5 > 0:
+                rd_recip(r - 1)
             rd_nb(r, 1)
             E(*MS(r + 2))
             rd_exp(r, 1)
@@ -257,13 +264,11 @@ def tile_contextualattention_t_kernel(tc, left, right, mid, sc00, sc01, sc10, sc
             Q(*ls)
             if r < 9:
                 rd_mm(r + 1)
-            T(*LS(r + 3))
-            if r % 5 > 0:
-                rd_recip(r - 1)
+            T(*LS(r + 1))
             for f in late:
                 f()
             if r % 5 > 0:
-                rd_norm(r - 1, 0, 1 if h == 0 else 4)
+                rd_norm(r - 1, 0, 4 if r - 1 in WIDE else 1)
 
         def c(x, h, q):
             return lambda: centers(x, h, q)
@@ -271,23 +276,21 @@ def tile_contextualattention_t_kernel(tc, left, right, mid, sc00, sc01, sc10, sc
         def a(x, h, q):
             return lambda: assemble(x, h, q, q + 1)
 
-        def n(r, q0, q1):
-            return lambda: rd_norm(r, q0, q1)
-
-        T(*LS(0))
-        T(*MS(0))
-        E(*LS(0))
-        E(*MS(0))
-        T(*LS(1))
-        Q(*LS(0))
-        Q(*MS(0))
-        E(*LS(1))
-        prep_z(MS(0)[0])
-        T(*MS(1))
+        WIDE = (0, 1)
+        T(L(0), L(1), L(2), L(3))
+        E(L(0), L(1), L(2), L(3))
+        T(M(0, 0))
+        Q(L(0), L(1))
+        T(L(4))
+        Q(L(2), L(3))
+        E(M(0, 0), L(4))
+        Q(M(0, 0))
+        T(M(0, 1))
+        Q(L(4))
+        prep_z(M(0, 0))
         rd_mm(0)
-        E(*MS(1))
-        Q(*LS(1))
-        T(*LS(2))
+        E(M(0, 1))
+        T(*LS(0))
         for r in range(4):
             round_(r)
         round_(4, (), (c(0, 0, 0),))
@@ -297,17 +300,26 @@ def tile_contextualattention_t_kernel(tc, left, right, mid, sc00, sc01, sc10, sc
         centers(0, 0, 2)
         assemble(0, 0, 0, 1)
         for r in range(5):
-            rd_norm(r, 1, 4)
-        round_(5, (a(0, 0, 1),), (c(0, 0, 3), c(1, 0, 0), a(0, 0, 2)))
-        round_(6, (a(1, 0, 0),), (c(1, 0, 1), a(0, 0, 3), c(1, 0, 2)))
-        round_(7, (a(1, 0, 1),), (a(1, 0, 2), c(1, 0, 3)))
-        round_(8, (a(1, 0, 3),), (c(0, 1, 0), c(0, 1, 1)))
-        round_(9, (c(0, 1, 2),), (c(0, 1, 3),))
+            if r not in WIDE:
+                rd_norm(r, 1, 4, (1, 3))
+            if r == 3:
+                centers(1, 0, 0)
+        assemble(1, 0, 0, 1)
+        round_(5, (a(0, 0, 1),), (c(1, 0, 1), c(0, 0, 3)))
+        round_(6, (a(0, 0, 2),), (a(1, 0, 1), c(1, 0, 2)))
+        round_(7, (a(0, 0, 3),), (a(1, 0, 2), c(1, 0, 3)))
+        round_(8, (a(1, 0, 3),), ())
+        round_(9)
         rd_recip(9)
-        rd_norm(9, 0, 4)
+        centers(0, 1, 2)
+        rd_norm(9, 0, 1)
+        centers(0, 1, 3)
         assemble(0, 1, 0, 1)
         for q in range(4):
             if q < 3:
-                assemble(0, 1, q + 1, q + 2)
+                for r in range(5, 10):
+                    rd_norm(r, q + 1, q + 2, ())
             centers(1, 1, q)
+            if q < 3:
+                assemble(0, 1, q + 1, q + 2)
             assemble(1, 1, q, q + 1)

@@ -19,7 +19,9 @@ BYTES = 2 * 256 * 256 * 30 * 4 + 2 * 256 * 256 * 20 * 2 + 2 * 256 * 256 * 10 * 2
 RUN = 2
 NQ = 4
 QO = 64
-V_EXITS = (1, 3)
+GM = 2
+MB = 3
+V_EXITS = (("L", 1, 0),)
 V_GROUPS = 8
 
 
@@ -33,7 +35,7 @@ def tile_contextualattention_t_kernel(tc, left, right, mid, sc00, sc01, sc10, sc
         srcp = ctx.enter_context(tc.tile_pool(name="srcp", bufs=2))
         keep = ctx.enter_context(tc.tile_pool(name="keep", bufs=1))
         gp = ctx.enter_context(tc.tile_pool(name="gp", bufs=2))
-        mp = ctx.enter_context(tc.tile_pool(name="mp", bufs=3))
+        mp = ctx.enter_context(tc.tile_pool(name="mp", bufs=MB))
         small = ctx.enter_context(tc.tile_pool(name="small", bufs=6))
         stat = ctx.enter_context(tc.tile_pool(name="stat", bufs=2))
         xtp = ctx.enter_context(tc.psum_pool(name="xtp", bufs=4))
@@ -89,14 +91,14 @@ def tile_contextualattention_t_kernel(tc, left, right, mid, sc00, sc01, sc10, sc
         def prep_e(unit):
             kind, a, b = unit
             xt = state[("xt", unit)]
+            eng_copy = nc.vector.tensor_copy if unit in V_EXITS else nc.scalar.copy
             if kind == "L":
                 g = gp.tile([P, 1024], BF16, tag="g_lc", name="g_lc", align_bytes=64, bufs=4)
-                eng_copy = nc.vector.tensor_copy if a in V_EXITS else nc.scalar.copy
                 eng_copy(out=g[:].bitcast(F32).rearrange("p (o u) -> p o u", u=2), in_=xt[:].rearrange("p u o -> p o u"))
             else:
-                g = gp.tile([P, 1024], BF16, tag="g_mid", name="g_mid", align_bytes=64)
+                g = gp.tile([P, 1024], BF16, tag="g_mid", name="g_mid", align_bytes=64, bufs=GM)
                 gw = g[:].bitcast(F32).rearrange("p (x b u) -> p x b u", x=2, u=2)
-                nc.scalar.copy(out=gw, in_=xt[:].rearrange("p x u b -> p x b u"))
+                eng_copy(out=gw, in_=xt[:].rearrange("p x u b -> p x b u"))
             state[("g", unit)] = g
 
         def prep_q(unit):
@@ -163,15 +165,15 @@ def tile_contextualattention_t_kernel(tc, left, right, mid, sc00, sc01, sc10, sc
                     accum_out=sums[:, 2 * i + t:2 * i + t + 1],
                 )
 
-        def rd_recip(s):
+        def rd_recip(s, j0=0, j1=4):
             h, k = divmod(s, 5)
             src_t, sums, rinv = state[("half", h)]
-            nc.vector.reciprocal(out=rinv[:, 4 * k:4 * k + 4], in_=sums[:, 4 * k:4 * k + 4])
+            nc.vector.reciprocal(out=rinv[:, 4 * k + j0:4 * k + j1], in_=sums[:, 4 * k + j0:4 * k + j1])
 
-        def rd_norm(s, q0, q1, on_scalar=()):
+        def rd_norm(s, q0, q1, on_scalar=(), j0=0, j1=4):
             h, k = divmod(s, 5)
             src_t, sums, rinv = state[("half", h)]
-            for j in range(4 * k, 4 * k + 4):
+            for j in range(4 * k + j0, 4 * k + j1):
                 i, t = divmod(j, 2)
                 rows = src_t[:, q0:q1, i, t, :]
                 if j % 4 in on_scalar:
@@ -193,22 +195,35 @@ def tile_contextualattention_t_kernel(tc, left, right, mid, sc00, sc01, sc10, sc
                 in_=scv[:, q, :, :, 0:10].rearrange("p y o (g e) -> p g y o e", e=2),
             )
 
-        def out_tile(n):
-            if n == 1:
-                return ins.tile([P, QO * 30], F32, tag="o_s", name="o_s")
-            return slots.tile([P, n * QO * 30], F32, tag="slot", name="o_t")
+        def interleave(x, h, q, cols, a0, a1, a2):
+            dst = cols.rearrange("p (a e y j) -> p a y j e", e=RUN, y=2, j=30)
+            srcv = state[("half", h)][0][:, q].rearrange("p i r (y a e) -> p a y (i r) e", y=2, e=RUN)
+            nc.vector.tensor_copy(out=dst[:, a0:a1], in_=srcv[:, a0:a1])
+            nc.scalar.copy(out=dst[:, a1:a2], in_=srcv[:, a1:a2])
 
-        def assemble(x, h, q0, q1):
-            src_t = state[("half", h)][0]
-            o_t = out_tile(q1 - q0)
-            dst = o_t[:].rearrange("p (q a e y j) -> p q a y j e", q=q1 - q0, e=RUN, y=2, j=30)
-            for q in range(q0, q1):
-                srcv = src_t[:, q].rearrange("p i r (y a e) -> p a y (i r) e", y=2, e=RUN)
-                nc.vector.tensor_copy(out=dst[:, q - q0, 0:V_GROUPS], in_=srcv[:, 0:V_GROUPS])
-                nc.scalar.copy(out=dst[:, q - q0, V_GROUPS:], in_=srcv[:, V_GROUPS:])
-            nc.sync.dma_start(
-                out=outs[x][h * P:(h + 1) * P, q0 * QO:q1 * QO, :].rearrange("b o j -> b (o j)"), in_=o_t[:]
-            )
+        def store(x, h, o0, cols):
+            rows = outs[x][h * P:(h + 1) * P, o0:o0 + cols.shape[1] // 30, :]
+            nc.sync.dma_start(out=rows.rearrange("b o j -> b (o j)"), in_=cols)
+
+        def assemble(x, h, q):
+            o_t = ins.tile([P, QO * 30], F32, tag="o_s", name="o_s")
+            interleave(x, h, q, o_t[:], 0, V_GROUPS, 16)
+            store(x, h, q * QO, o_t[:])
+
+        def assemble_cut(x, h, q):
+            o_t = ins.tile([P, QO * 30], F32, tag="o_s", name="o_s")
+            for a0, a1, a2 in ((0, 4, 6), (6, 10, 16)):
+                r0, r1 = a0 * 2 * RUN, a2 * 2 * RUN
+                interleave(x, h, q, o_t[:], a0, a1, a2)
+                store(x, h, q * QO + r0, o_t[:, r0 * 30:r1 * 30])
+
+        def assemble_pair(x, h, q, part):
+            if part == 0:
+                state[("pair", x, h)] = slots.tile([P, 2 * QO * 30], F32, tag="slot", name="o_t")
+            o_t = state[("pair", x, h)]
+            interleave(x, h, q + part, o_t[:, part * QO * 30:(part + 1) * QO * 30], 0, V_GROUPS, 16)
+            if part == 1:
+                store(x, h, q * QO, o_t[:])
 
         def L(i):
             return ("L", i, 0)
@@ -274,7 +289,7 @@ def tile_contextualattention_t_kernel(tc, left, right, mid, sc00, sc01, sc10, sc
             return lambda: centers(x, h, q)
 
         def a(x, h, q):
-            return lambda: assemble(x, h, q, q + 1)
+            return lambda: assemble(x, h, q)
 
         WIDE = (0, 1)
         T(L(0), L(1), L(2), L(3))
@@ -295,31 +310,39 @@ def tile_contextualattention_t_kernel(tc, left, right, mid, sc00, sc01, sc10, sc
             round_(r)
         round_(4, (), (c(0, 0, 0),))
         rd_recip(4)
-        centers(0, 0, 1)
+        centers(0, 0, 1, nc.scalar.copy)
         rd_norm(4, 0, 1)
         centers(0, 0, 2)
-        assemble(0, 0, 0, 1)
+        assemble(0, 0, 0)
         for r in range(5):
             if r not in WIDE:
                 rd_norm(r, 1, 4, (1, 3))
             if r == 3:
                 centers(1, 0, 0)
-        assemble(1, 0, 0, 1)
+        assemble(1, 0, 0)
         round_(5, (a(0, 0, 1),), (c(1, 0, 1), c(0, 0, 3)))
         round_(6, (a(0, 0, 2),), (a(1, 0, 1), c(1, 0, 2)))
         round_(7, (a(0, 0, 3),), (a(1, 0, 2), c(1, 0, 3)))
         round_(8, (a(1, 0, 3),), ())
         round_(9)
-        rd_recip(9)
+        rd_recip(9, 0, 2)
         centers(0, 1, 2)
-        rd_norm(9, 0, 1)
+        rd_norm(9, 0, 1, (), 0, 2)
+        rd_recip(9, 2, 4)
         centers(0, 1, 3)
-        assemble(0, 1, 0, 1)
+        rd_norm(9, 0, 1, (), 2, 4)
+        assemble_cut(0, 1, 0)
         for q in range(4):
             if q < 3:
-                for r in range(5, 10):
-                    rd_norm(r, q + 1, q + 2, ())
+                for r in range(5, 7):
+                    rd_norm(r, q + 1, q + 2)
             centers(1, 1, q)
+            if q < 2:
+                assemble(1, 1, q)
+            else:
+                assemble_pair(1, 1, 2, q - 2)
             if q < 3:
-                assemble(0, 1, q + 1, q + 2)
-            assemble(1, 1, q, q + 1)
+                for r in range(7, 10):
+                    rd_norm(r, q + 1, q + 2)
+            if q < 3:
+                assemble(0, 1, q + 1)

@@ -191,8 +191,8 @@ def tile_contextualattention_t_kernel(tc, left, right, mid, sc00, sc01, sc10, sc
             src_t = state[("half", h)][0]
             scv = sc_sb[(x, h)][:].rearrange("p (q o y l) -> p q y o l", q=NQ, y=2, l=30)
             copy(
-                out=src_t[:, q, :, 2, :].rearrange("p (g e) (y o) -> p g y o e", e=2, y=2),
-                in_=scv[:, q, :, :, 0:10].rearrange("p y o (g e) -> p g y o e", e=2),
+                out=src_t[:, q, :, 2, :].rearrange("p (g e) (y o) -> p y g o e", e=2, y=2),
+                in_=scv[:, q, :, :, 0:10].rearrange("p y o (g e) -> p y g o e", e=2),
             )
 
         def interleave(x, h, q, cols, a0, a1, a2):
@@ -283,7 +283,7 @@ def tile_contextualattention_t_kernel(tc, left, right, mid, sc00, sc01, sc10, sc
             for f in late:
                 f()
             if r % 5 > 0:
-                rd_norm(r - 1, 0, 4 if r - 1 in WIDE else 1)
+                rd_norm(r - 1, 0, 2 if r < 5 else 1)
 
         def c(x, h, q):
             return lambda: centers(x, h, q)
@@ -291,7 +291,6 @@ def tile_contextualattention_t_kernel(tc, left, right, mid, sc00, sc01, sc10, sc
         def a(x, h, q):
             return lambda: assemble(x, h, q)
 
-        WIDE = (0, 1)
         T(L(0), L(1), L(2), L(3))
         E(L(0), L(1), L(2), L(3))
         T(M(0, 0))
@@ -311,12 +310,11 @@ def tile_contextualattention_t_kernel(tc, left, right, mid, sc00, sc01, sc10, sc
         round_(4, (), (c(0, 0, 0),))
         rd_recip(4)
         centers(0, 0, 1, nc.scalar.copy)
-        rd_norm(4, 0, 1)
+        rd_norm(4, 0, 2)
         centers(0, 0, 2)
         assemble(0, 0, 0)
         for r in range(5):
-            if r not in WIDE:
-                rd_norm(r, 1, 4, (1, 3))
+            rd_norm(r, 2, 4, (1, 3))
             if r == 3:
                 centers(1, 0, 0)
         assemble(1, 0, 0)

@@ -205,14 +205,14 @@ def tile_contextualattention_t_kernel(tc, left, right, mid, sc00, sc01, sc10, sc
             rows = outs[x][h * P:(h + 1) * P, o0:o0 + cols.shape[1] // 30, :]
             nc.sync.dma_start(out=rows.rearrange("b o j -> b (o j)"), in_=cols)
 
-        def assemble(x, h, q):
+        def assemble(x, h, q, v=V_GROUPS):
             o_t = ins.tile([P, QO * 30], F32, tag="o_s", name="o_s")
-            interleave(x, h, q, o_t[:], 0, V_GROUPS, 16)
+            interleave(x, h, q, o_t[:], 0, v, 16)
             store(x, h, q * QO, o_t[:])
 
         def assemble_cut(x, h, q):
             o_t = ins.tile([P, QO * 30], F32, tag="o_s", name="o_s")
-            for a0, a1, a2 in ((0, 4, 6), (6, 10, 16)):
+            for a0, a1, a2 in ((0, 4, 6), (6, 12, 16)):
                 r0, r1 = a0 * 2 * RUN, a2 * 2 * RUN
                 interleave(x, h, q, o_t[:], a0, a1, a2)
                 store(x, h, q * QO + r0, o_t[:, r0 * 30:r1 * 30])
@@ -268,7 +268,7 @@ def tile_contextualattention_t_kernel(tc, left, right, mid, sc00, sc01, sc10, sc
             for u in MS(r + 1):
                 prep_z(u)
             if r == 9:
-                centers(0, 1, 1)
+                rd_norm(5, 1, 2)
             if r % 5 > 0:
                 rd_recip(r - 1)
             rd_nb(r, 1)
@@ -324,23 +324,26 @@ def tile_contextualattention_t_kernel(tc, left, right, mid, sc00, sc01, sc10, sc
         round_(8, (a(1, 0, 3),), ())
         round_(9)
         rd_recip(9, 0, 2)
-        centers(0, 1, 2)
+        rd_norm(6, 1, 2)
         rd_norm(9, 0, 1, (), 0, 2)
         rd_recip(9, 2, 4)
-        centers(0, 1, 3)
+        rd_norm(7, 1, 2)
         rd_norm(9, 0, 1, (), 2, 4)
         assemble_cut(0, 1, 0)
         for q in range(4):
-            if q < 3:
-                for r in range(5, 7):
+            if 0 < q < 3:
+                for r in range(5, 8):
                     rd_norm(r, q + 1, q + 2)
+            if q == 0:
+                centers(0, 1, 1)
             centers(1, 1, q)
             if q < 2:
-                assemble(1, 1, q)
+                assemble(1, 1, q, 10 if q == 0 else V_GROUPS)
             else:
                 assemble_pair(1, 1, 2, q - 2)
             if q < 3:
-                for r in range(7, 10):
+                if q > 0:
+                    centers(0, 1, q + 1)
+                for r in range(8, 10):
                     rd_norm(r, q + 1, q + 2)
-            if q < 3:
                 assemble(0, 1, q + 1)

from contextlib import ExitStack

import concourse.mybir as mybir
from concourse.masks import make_identity

F32 = mybir.dt.float32
BF16 = mybir.dt.bfloat16
U32 = mybir.dt.uint32
U8 = mybir.dt.uint8
FP8X4 = mybir.dt.float8_e4m3fn_x4
ACT = mybir.ActivationFunctionType
AX = mybir.AxisListType

P = 128
NCHUNK = 10
FLOPS = 2 * 5120 * 256 * 512
BYTES = 2 * 256 * 256 * 30 * 4 + 2 * 256 * 256 * 20 * 2 + 2 * 256 * 256 * 10 * 2

RUN = 2
NQ = 4
QO = 64
GM = 2
MB = 3
V_EXITS = (("L", 1, 0),)
V_GROUPS = 8


def tile_contextualattention_t_kernel(tc, left, right, mid, sc00, sc01, sc10, sc11, out_0, out_1):
    nc = tc.nc
    outs = (out_0, out_1)
    with ExitStack() as ctx:
        const = ctx.enter_context(tc.tile_pool(name="const", bufs=1))
        ins = ctx.enter_context(tc.tile_pool(name="ins", bufs=4))
        slots = ctx.enter_context(tc.tile_pool(name="slots", bufs=4))
        srcp = ctx.enter_context(tc.tile_pool(name="srcp", bufs=2))
        keep = ctx.enter_context(tc.tile_pool(name="keep", bufs=1))
        gp = ctx.enter_context(tc.tile_pool(name="gp", bufs=2))
        mp = ctx.enter_context(tc.tile_pool(name="mp", bufs=MB))
        small = ctx.enter_context(tc.tile_pool(name="small", bufs=6))
        stat = ctx.enter_context(tc.tile_pool(name="stat", bufs=2))
        xtp = ctx.enter_context(tc.psum_pool(name="xtp", bufs=4))
        scp = ctx.enter_context(tc.psum_pool(name="scp", bufs=4))

        ident = const.tile([P, P], F32, name="ident")
        make_identity(nc, ident[:])
        ctx.enter_context(tc.manual_schedule())

        left_sb = ins.tile([P, 2, 2560], BF16, tag="in10", name="left_sb")
        right_sb = ins.tile([P, 2, 2560], BF16, tag="in10", name="right_sb")
        mid_sb = [ins.tile([P, 5120], BF16, tag="in10", name="mid_sb%d" % h) for h in range(2)]
        nc.sync.dma_start(out=left_sb[:], in_=left.rearrange("(q o) c l -> o q (c l)", q=2))
        nc.sync.dma_start(out=mid_sb[0][:], in_=mid[0:P].rearrange("b c l -> b (c l)"))
        nc.sync.dma_start(out=right_sb[:], in_=right.rearrange("(q o) c l -> o q (c l)", q=2))
        sc_sb = {}

        def load_sc(x, h):
            t = slots.tile([P, 7680], BF16, tag="slot", name="sc_sb%d%d" % (x, h))
            sc = (sc00, sc10)[x]
            nc.sync.dma_start(out=t[:], in_=sc[h * P:(h + 1) * P].rearrange("b c l -> b (c l)"))
            sc_sb[(x, h)] = t

        load_sc(0, 0)
        nc.sync.dma_start(out=mid_sb[1][:], in_=mid[P:2 * P].rearrange("b c l -> b (c l)"))
        load_sc(1, 0)
        load_sc(0, 1)
        load_sc(1, 1)

        lc_codes = keep.tile([P, NCHUNK, 256], U32, name="lc_codes", align_bytes=64)
        lc_scales = keep.tile([P, NCHUNK, 256], U8, name="lc_scales", align_bytes=64)
        zero_tap = keep.tile([P, 2 * 5, 256], U32, name="zero_tap", align_bytes=64)
        nc.gpsimd.memset(zero_tap[:], 0)
        state = {}

        def prep_t(unit):
            kind, a, b = unit
            if kind == "L":
                sb = left_sb if a < 5 else right_sb
                words = sb[:].bitcast(F32).rearrange("p q (m u i) -> p q m u i", u=2, i=5)
                xt = xtp.tile([P, 2, 256], F32, tag="xt", name="xt_lc")
                for q in range(2):
                    for u in range(2):
                        nc.tensor.transpose(out=xt[:, u, q * P:(q + 1) * P], in_=words[:, q, :, u, a % 5], identity=ident[:])
            else:
                words = mid_sb[a][:].bitcast(F32).rearrange("p (m u i) -> p m u i", u=2, i=10)
                xt = xtp.tile([P, 2, 2, P], F32, tag="xt", name="xt_mid")
                for x in range(2):
                    for u in range(2):
                        nc.tensor.transpose(out=xt[:, x, u, :], in_=words[:, :, u, 2 * b + x], identity=ident[:])
            state[("xt", unit)] = xt

        def prep_e(unit):
            kind, a, b = unit
            xt = state[("xt", unit)]
            eng_copy = nc.vector.tensor_copy if unit in V_EXITS else nc.scalar.copy
            if kind == "L":
                g = gp.tile([P, 1024], BF16, tag="g_lc", name="g_lc", align_bytes=64, bufs=4)
                eng_copy(out=g[:].bitcast(F32).rearrange("p (o u) -> p o u", u=2), in_=xt[:].rearrange("p u o -> p o u"))
            else:
                g = gp.tile([P, 1024], BF16, tag="g_mid", name="g_mid", align_bytes=64, bufs=GM)
                gw = g[:].bitcast(F32).rearrange("p (x b u) -> p x b u", x=2, u=2)
                eng_copy(out=gw, in_=xt[:].rearrange("p x u b -> p x b u"))
            state[("g", unit)] = g

        def prep_q(unit):
            kind, a, b = unit
            g = state[("g", unit)]
            if kind == "L":
                nc.vector.quantize_mx(out=lc_codes[:, a, :].bitcast(FP8X4), scales=lc_scales[:, a, :], in_=g[:])
            else:
                codes = mp.tile([P, 256], U32, tag="m_codes", name="m_codes", align_bytes=64)
                scales = mp.tile([P, 256], U8, tag="m_scales", name="m_scales", align_bytes=64)
                nc.vector.quantize_mx(out=codes[:].bitcast(FP8X4), scales=scales[:], in_=g[:])
                state[("m", a, b)] = (codes, scales)

        def prep_z(unit):
            kind, a, b = unit
            codes = state[("m", a, b)][0]
            nc.vector.tensor_copy(
                out=zero_tap[:, 5 * a + b, :].bitcast(U8).rearrange("p (n e) -> p n e", e=2)[:, :, 1],
                in_=codes[:].bitcast(U8).rearrange("p (n e) -> p n e", e=2)[:, :, 0],
            )

        def rd_mm(s):
            h, k = divmod(s, 5)
            codes, scales = state[("m", h, k)]
            late = zero_tap[:, 5 * h + k, :]
            for x in range(2):
                state[("ps", s, x)] = scp.tile([P, 2, 256], F32, tag="ps", name="ps")
            for t, words in ((1, codes), (0, late)):
                for x in range(2):
                    i = 2 * k + x
                    nc.tensor.matmul_mx(
                        out=state[("ps", s, x)][:, t, :],
                        lhsT=words[:, x * P:(x + 1) * P].bitcast(FP8X4),
                        lhsT_scale=scales[:, x * P:(x + 1) * P],
                        rhs=lc_codes[:, i, :].bitcast(FP8X4),
                        rhs_scale=lc_scales[:, i, :],
                        start=True,
                        stop=True,
                    )

        def rd_max(s, x):
            mx = small.tile([P, 2], F32, tag="mx", name="mx")
            nc.vector.reduce_max(out=mx[:], in_=state[("ps", s, x)][:], axis=AX.X)
            state[("mx", s, x)] = mx

        def rd_nb(s, x):
            nb = small.tile([P, 2], F32, tag="nb", name="nb")
            nc.vector.tensor_scalar_mul(out=nb[:], in0=state[("mx", s, x)][:], scalar1=-10.0)
            state[("nb", s, x)] = nb

        def rd_exp(s, x):
            h, k = divmod(s, 5)
            src_t, sums, rinv = state[("half", h)]
            nb = state[("nb", s, x)]
            i = 2 * k + x
            ps = state[("ps", s, x)]
            for t in range(2):
                nc.scalar.activation(
                    out=src_t[:, :, i, t, :].rearrange("p q (y o) -> p q y o", y=2),
                    in_=ps[:, t, :].rearrange("p (q o y) -> p q y o", q=NQ, y=2),
                    func=ACT.Exp,
                    bias=nb[:, t:t + 1],
                    scale=10.0,
                    accum_out=sums[:, 2 * i + t:2 * i + t + 1],
                )

        def rd_recip(s, j0=0, j1=4):
            h, k = divmod(s, 5)
            src_t, sums, rinv = state[("half", h)]
            nc.vector.reciprocal(out=rinv[:, 4 * k + j0:4 * k + j1], in_=sums[:, 4 * k + j0:4 * k + j1])

        def rd_norm(s, q0, q1, on_scalar=(), j0=0, j1=4):
            h, k = divmod(s, 5)
            src_t, sums, rinv = state[("half", h)]
            for j in range(4 * k + j0, 4 * k + j1):
                i, t = divmod(j, 2)
                rows = src_t[:, q0:q1, i, t, :]
                if j % 4 in on_scalar:
                    nc.scalar.activation(out=rows, in_=rows, func=ACT.Copy, scale=rinv[:, j:j + 1])
                else:
                    nc.vector.tensor_scalar_mul(out=rows, in0=rows, scalar1=rinv[:, j:j + 1])

        def new_half(h):
            src_t = srcp.tile([P, NQ, NCHUNK, 3, QO], F32, tag="src", name="src_t")
            sums = stat.tile([P, 2 * NCHUNK], F32, tag="sums", name="sums")
            rinv = stat.tile([P, 2 * NCHUNK], F32, tag="rinv", name="rinv")
            state[("half", h)] = (src_t, sums, rinv)

        def centers(x, h, q, copy=nc.vector.tensor_copy):
            src_t = state[("half", h)][0]
            scv = sc_sb[(x, h)][:].rearrange("p (q o y l) -> p q y o l", q=NQ, y=2, l=30)
            copy(
                out=src_t[:, q, :, 2, :].rearrange("p (g e) (y o) -> p y g o e", e=2, y=2),
                in_=scv[:, q, :, :, 0:10].rearrange("p y o (g e) -> p y g o e", e=2),
            )

        def interleave(x, h, q, cols, a0, a1, a2):
            dst = cols.rearrange("p (a e y j) -> p a y j e", e=RUN, y=2, j=30)
            srcv = state[("half", h)][0][:, q].rearrange("p i r (y a e) -> p a y (i r) e", y=2, e=RUN)
            nc.vector.tensor_copy(out=dst[:, a0:a1], in_=srcv[:, a0:a1])
            nc.scalar.copy(out=dst[:, a1:a2], in_=srcv[:, a1:a2])

        def store(x, h, o0, cols):
            rows = outs[x][h * P:(h + 1) * P, o0:o0 + cols.shape[1] // 30, :]
            nc.sync.dma_start(out=rows.rearrange("b o j -> b (o j)"), in_=cols)

        def assemble(x, h, q, v=V_GROUPS):
            o_t = ins.tile([P, QO * 30], F32, tag="o_s", name="o_s")
            interleave(x, h, q, o_t[:], 0, v, 16)
            store(x, h, q * QO, o_t[:])

        def assemble_cut(x, h, q):
            o_t = ins.tile([P, QO * 30], F32, tag="o_s", name="o_s")
            for a0, a1, a2 in ((0, 4, 6), (6, 12, 16)):
                r0, r1 = a0 * 2 * RUN, a2 * 2 * RUN
                interleave(x, h, q, o_t[:], a0, a1, a2)
                store(x, h, q * QO + r0, o_t[:, r0 * 30:r1 * 30])

        def assemble_pair(x, h, q, part):
            if part == 0:
                state[("pair", x, h)] = slots.tile([P, 2 * QO * 30], F32, tag="slot", name="o_t")
            o_t = state[("pair", x, h)]
            interleave(x, h, q + part, o_t[:, part * QO * 30:(part + 1) * QO * 30], 0, V_GROUPS, 16)
            if part == 1:
                store(x, h, q * QO, o_t[:])

        def L(i):
            return ("L", i, 0)

        def M(h, k):
            return ("M", h, k)

        def T(*us):
            for u in us:
                prep_t(u)

        def E(*us):
            for u in us:
                prep_e(u)

        def Q(*us):
            for u in us:
                prep_q(u)

        new_half(0)
        new_half(1)

        def LS(r):
            return [[L(5)], [L(6), L(7)], [L(8), L(9)]][r] if r < 3 else []

        def MS(r):
            return [M(r // 5, r % 5)] if r < 10 else []

        def round_(r, early=(), late=()):
            ls = LS(r)
            E(*ls)
            rd_max(r, 0)
            Q(*MS(r + 1))
            if r == 9:
                centers(0, 1, 0)
            rd_nb(r, 0)
            T(*MS(r + 2))
            for f in early[:1]:
                f()
            rd_exp(r, 0)
            rd_max(r, 1)
            for u in MS(r + 1):
                prep_z(u)
            if r == 9:
                rd_norm(5, 1, 2)
            if r % 5 > 0:
                rd_recip(r - 1)
            rd_nb(r, 1)
            E(*MS(r + 2))
            rd_exp(r, 1)
            for f in early[1:]:
                f()
            Q(*ls)
            if r < 9:
                rd_mm(r + 1)
            T(*LS(r + 1))
            for f in late:
                f()
            if r % 5 > 0:
                rd_norm(r - 1, 0, 2 if r < 5 else 1)

        def c(x, h, q):
            return lambda: centers(x, h, q)

        def a(x, h, q):
            return lambda: assemble(x, h, q)

        T(L(0), L(1), L(2), L(3))
        E(L(0), L(1), L(2), L(3))
        T(M(0, 0))
        Q(L(0), L(1))
        T(L(4))
        Q(L(2), L(3))
        E(M(0, 0), L(4))
        Q(M(0, 0))
        T(M(0, 1))
        Q(L(4))
        prep_z(M(0, 0))
        rd_mm(0)
        E(M(0, 1))
        T(*LS(0))
        for r in range(4):
            round_(r)
        round_(4, (), (c(0, 0, 0),))
        rd_recip(4)
        centers(0, 0, 1, nc.scalar.copy)
        rd_norm(4, 0, 2)
        centers(0, 0, 2)
        assemble(0, 0, 0)
        for r in range(5):
            rd_norm(r, 2, 4, (1, 3))
            if r == 3:
                centers(1, 0, 0)
        assemble(1, 0, 0)
        round_(5, (a(0, 0, 1),), (c(1, 0, 1), c(0, 0, 3)))
        round_(6, (a(0, 0, 2),), (a(1, 0, 1), c(1, 0, 2)))
        round_(7, (a(0, 0, 3),), (a(1, 0, 2), c(1, 0, 3)))
        round_(8, (a(1, 0, 3),), ())
        round_(9)
        rd_recip(9, 0, 2)
        rd_norm(6, 1, 2)
        rd_norm(9, 0, 1, (), 0, 2)
        rd_recip(9, 2, 4)
        rd_norm(7, 1, 2)
        rd_norm(9, 0, 1, (), 2, 4)
        assemble_cut(0, 1, 0)
        for q in range(4):
            if 0 < q < 3:
                for r in range(5, 8):
                    rd_norm(r, q + 1, q + 2)
            if q == 0:
                centers(0, 1, 1)
            centers(1, 1, q)
            if q < 2:
                assemble(1, 1, q, 10 if q == 0 else V_GROUPS)
            else:
                assemble_pair(1, 1, 2, q - 2)
            if q < 3:
                if q > 0:
                    centers(0, 1, q + 1)
                for r in range(8, 10):
                    rd_norm(r, q + 1, q + 2)
                assemble(0, 1, q + 1)
